import numpy as np
import ml_dtypes


def mxq(x, axis, fmt="e4m3"):
    dtype, down = {"e4m3": (ml_dtypes.float8_e4m3fn, 7), "e5m2": (ml_dtypes.float8_e5m2, 14)}[fmt]
    v = np.moveaxis(np.asarray(x, np.float32).astype(ml_dtypes.bfloat16).astype(np.float64), axis, -1)
    blocks = v.reshape(v.shape[:-1] + (-1, 32))
    amax = np.abs(blocks).max(-1, keepdims=True)
    byte = np.maximum(np.where(amax > 0, np.frexp(amax)[1] - 1 + 127, 0) - down, 1)
    scale = np.exp2(byte - 127.0)
    codes = (blocks / scale).astype(np.float32).astype(dtype).astype(np.float64)
    return np.moveaxis((codes * scale).reshape(v.shape), -1, axis)


WIDE = False


def mx_kscale(k):
    if not WIDE:
        return np.ones(k)
    levels = np.array([10, -10, 5, -5, 0])
    if k % 512:
        return np.exp2(np.random.permutation(np.resize(levels, k // 32))).repeat(32)
    a = np.empty((k // 512, 16))
    for p in range(k // 512):
        a[p, :8] = np.random.permutation(np.resize(levels, 8))
        for g in range(8):
            far = levels[np.abs(levels - a[p, g]) >= 10]
            a[p, g + 8] = far[np.random.randint(len(far))]
    return np.exp2(a.ravel()).repeat(32)


BF16 = ml_dtypes.bfloat16


def bf(x):
    return np.asarray(x, np.float32).astype(BF16)


def f64(x):
    return np.asarray(x).astype(np.float64)


B, H, S, D, QB = 1, 2, 2048, 128, 512


def setup_inputs():
    t = mx_kscale(S)
    t = t / t.max()
    t[:32] = 1.0
    q = np.random.standard_normal((B, H, S, D)) * 1.5
    k = np.random.standard_normal((B, H, S, D))
    v = np.random.standard_normal((B, H, S, D)) * 2.0
    q[..., 0] = np.log(2.0) * np.sqrt(D)
    k[..., 0] += np.log2(t)
    v = v / t[:, None]
    return {"q": bf(q), "k": bf(k), "v": bf(v), "is_causal": 1}


def reference(q, k, v, is_causal):
    q, k = f64(q), f64(k)
    vq = mxq(f64(v), 2, "e4m3")
    out = []
    for q0 in range(0, S, QB):
        n = q0 + QB if is_causal else S
        s = q[:, :, q0:q0 + QB] @ k[:, :, :n].transpose(0, 1, 3, 2) / np.sqrt(D)
        if is_causal:
            s = np.where(np.arange(n)[None, :] > np.arange(q0, q0 + QB)[:, None], -np.inf, s)
        e = np.exp(s - s.max(-1, keepdims=True))
        out.append((mxq(e, 3, "e4m3") @ vq[:, :, :n]) / e.sum(-1, keepdims=True))
    return np.concatenate(out, 2)

@@ -1,0 +1,374 @@
+from contextlib import ExitStack
+
+import concourse.masks as masks
+import concourse.mybir as mybir
+
+F32 = mybir.dt.float32
+BF16 = mybir.dt.bfloat16
+U32 = mybir.dt.uint32
+U8 = mybir.dt.uint8
+FP8X4 = mybir.dt.float8_e4m3fn_x4
+ALU = mybir.AluOpType
+ACT = mybir.ActivationFunctionType
+AX = mybir.AxisListType
+
+P = 128
+H = 2
+S = 2048
+D = 128
+NT = S // P
+PASS = 512
+SCALE = 1.0 / (D ** 0.5)
+MASK_VALUE = -1.0e30
+FLOPS = 4 * H * D * sum(PASS * PASS * (i + 1) for i in range(S // PASS))
+
+MANUAL = True
+LOOKAHEAD = 3
+S_BANKS = 4
+XT_BANKS = 2
+PV_BANKS = 2
+V_COPY_NPASS = 1
+OUT_LAG = 1
+PLANE_BUFS = 2
+GG_BUFS = 1
+G_KEEP = 1
+PREP_ON_S = 0
+V_DIRECT_MOD = 0
+VREG_G = 0
+AHEAD = 2
+BEHIND = 3
+SNEG_BUFS = 4
+GRP_BUFS = 4
+
+
+def tile_scaleddotproductattention_kernel(tc, q, k, v, is_causal, out):
+    nc = tc.nc
+    assert is_causal == 1
+    q_v = q.rearrange("b h (c p) d -> (b h) p c d", p=P)
+    k_v = k.rearrange("b h (c p) d -> (b h) p c d", p=P)
+    v_v = v.rearrange("b h (g p t) d -> (b h) p g (t d)", p=P, t=4)
+    out_v = out.rearrange("b h (c p) d -> (b h) c p d", p=P)
+
+    with ExitStack() as ctx:
+        if MANUAL:
+            ctx.enter_context(tc.manual_schedule())
+        keep = ctx.enter_context(tc.tile_pool(name="keep", bufs=1))
+        sneg_pool = ctx.enter_context(tc.tile_pool(name="sneg", bufs=SNEG_BUFS))
+        grp_pool = ctx.enter_context(tc.tile_pool(name="grp", bufs=GRP_BUFS))
+        plane_pool = ctx.enter_context(tc.tile_pool(name="plane", bufs=PLANE_BUFS))
+        gg_pool = ctx.enter_context(tc.tile_pool(name="gg", bufs=GG_BUFS))
+        code_pool = ctx.enter_context(tc.tile_pool(name="code", bufs=3))
+        small = ctx.enter_context(tc.tile_pool(name="small", bufs=8))
+        out_pool = ctx.enter_context(tc.tile_pool(name="outp", bufs=4))
+        psum_s = ctx.enter_context(tc.psum_pool(name="ps_s", bufs=S_BANKS))
+        psum_x = ctx.enter_context(tc.psum_pool(name="ps_x", bufs=XT_BANKS))
+        psum_o = ctx.enter_context(tc.psum_pool(name="ps_o", bufs=PV_BANKS))
+
+        q_sb = [keep.tile([P, NT, D], BF16, name="q_sb%d" % h) for h in range(H)]
+        k_sb = [keep.tile([P, NT, D], BF16, name="k_sb%d" % h) for h in range(H)]
+        v_sb = [keep.tile([P, NT, D], BF16, name="v_sb%d" % h) for h in range(H)]
+        nc.sync.dma_start(out=k_sb[0][:, 0:4, :], in_=k_v[0][:, 0:4, :])
+        nc.sync.dma_start(out=q_sb[0][:, 0:4, :], in_=q_v[0][:, 0:4, :])
+        nc.sync.dma_start(out=k_sb[0][:, 4:8, :], in_=k_v[0][:, 4:8, :])
+        nc.sync.dma_start(out=q_sb[0][:, 4:8, :], in_=q_v[0][:, 4:8, :])
+        nc.sync.dma_start(out=v_sb[0][:].rearrange("p (g t) d -> p g (t d)", t=4), in_=v_v[0])
+        nc.sync.dma_start(out=k_sb[0][:, 8:NT, :], in_=k_v[0][:, 8:NT, :])
+        nc.sync.dma_start(out=q_sb[0][:, 8:NT, :], in_=q_v[0][:, 8:NT, :])
+        nc.sync.dma_start(out=k_sb[1][:], in_=k_v[1])
+        nc.sync.dma_start(out=q_sb[1][:], in_=q_v[1])
+        nc.sync.dma_start(out=v_sb[1][:].rearrange("p (g t) d -> p g (t d)", t=4), in_=v_v[1])
+
+        ident = keep.tile([P, P], BF16, name="ident")
+        masks.make_identity(nc, ident[:])
+        mask_f = keep.tile([P, P], F32, name="mask_f")
+        nc.gpsimd.memset(mask_f[:], 0.0)
+        nc.gpsimd.affine_select(
+            out=mask_f[:], in_=mask_f[:], compare_op=ALU.is_ge, fill=MASK_VALUE,
+            base=0, pattern=[[-1, P]], channel_multiplier=1,
+        )
+        mask_b = keep.tile([P, P], BF16, name="mask_b")
+        nc.vector.tensor_copy(out=mask_b[:], in_=mask_f[:])
+        warm = keep.tile([P, 1], F32, name="warm")
+        nc.vector.memset(warm[:], 0.0)
+        warm2 = keep.tile([P, 1], F32, name="warm2")
+        nc.scalar.activation(out=warm2[:], in_=warm[:], func=ACT.Exp)
+        e_cls = [keep.tile([P, S], BF16, name="e_cls%d" % c) for c in range(4 * H)]
+        for c in range(4 * H):
+            if c % 4 < 3:
+                nc.gpsimd.memset(e_cls[c][:, S - P * (3 - c % 4):S], 0.0)
+
+        q_t = [keep.tile([P, S], BF16, name="q_t%d" % h) for h in range(H)]
+        k_t = [keep.tile([P, S], BF16, name="k_t%d" % h) for h in range(H)]
+        v_grp = [keep.tile([P, 4, D, 4], BF16, name="v_grp%d" % h, align_bytes=64) for h in range(H)]
+        v_codes = [keep.tile([P, 4 * D], U32, name="v_codes%d" % h, align_bytes=64) for h in range(H)]
+        v_scales = [keep.tile([P, 4 * D], U8, name="v_scales%d" % h, align_bytes=64) for h in range(H)]
+
+        ready = set()
+        state = {}
+
+        def prep_job(kind, h, grp):
+            src = (k_sb if kind == "k" else q_sb)[h]
+            dst = (k_t if kind == "k" else q_t)[h]
+            box = {}
+
+            def pe():
+                ps = psum_s.tile([P, 4, P], BF16, name="prep_ps", tag="s")
+                box["ps"] = ps
+                for c in range(4):
+                    nc.tensor.transpose(out=ps[:, c, :], in_=src[:, 4 * grp + c, :], identity=ident[:])
+
+            def ve():
+                eng_copy = nc.scalar.copy if (PREP_ON_S and not (h == 0 and grp == 0)) else nc.vector.tensor_copy
+                eng_copy(
+                    out=dst[:, PASS * grp:PASS * (grp + 1)],
+                    in_=box["ps"][:].rearrange("p c x -> p (c x)"),
+                )
+                ready.add((kind, h, grp))
+
+            return (pe, ve)
+
+        def qk_job(x, h, t, b):
+            i = t // 4
+            n = P * (t + 1)
+            w = min(PASS, n - PASS * b)
+            box = {}
+
+            def pe():
+                assert ("q", h, i) in ready and all(("k", h, g) in ready for g in range(b + 1))
+                ps = psum_s.tile([P, PASS], F32, name="s_ps", tag="s")
+                box["ps"] = ps
+                q_cols = q_t[h][:, P * t:P * (t + 1)]
+                if b < i:
+                    nc.tensor.matmul(out=ps[:, :], lhsT=q_cols, rhs=k_t[h][:, PASS * b:PASS * (b + 1)], start=True, stop=True)
+                else:
+                    if w > P:
+                        nc.tensor.matmul(out=ps[:, 0:w - P], lhsT=q_cols, rhs=k_t[h][:, PASS * b:PASS * b + w - P], start=True, stop=True)
+                    nc.tensor.matmul(out=ps[:, w - P:w], lhsT=q_cols, rhs=k_t[h][:, n - P:n], start=True, stop=False)
+                    nc.tensor.matmul(out=ps[:, w - P:w], lhsT=ident[:], rhs=mask_b[:], start=False, stop=True)
+
+            def ve():
+                st = state[x]
+                if b == 0:
+                    st["sneg"] = sneg_pool.tile([P, S], F32, name="sneg")
+                    st["pm"] = small.tile([P, 4], F32, name="pm")
+                nc.vector.tensor_scalar(
+                    out=st["sneg"][:, PASS * b:PASS * b + w], in0=box["ps"][:, 0:w],
+                    scalar1=-SCALE, scalar2=None, op0=ALU.mult, op1=ALU.min,
+                    accum_out=st["pm"][:, b:b + 1],
+                )
+                if b == i:
+                    if i > 0:
+                        negm = small.tile([P, 1], F32, name="negm")
+                        nc.vector.tensor_reduce(out=negm[:], in_=st["pm"][:, 0:i + 1], axis=AX.X, op=ALU.min)
+                        st["negm"] = negm[:, 0:1]
+                    else:
+                        st["negm"] = st["pm"][:, 0:1]
+
+            return (pe, ve)
+
+        seq = [(0, t) for t in range(NT)] + [(1, t) for t in range(NT - 1, -1, -1)]
+        NX = len(seq)
+        prep_before = {
+            2: [("k", 0, 1), ("q", 0, 1)],
+            6: [("k", 0, 2), ("q", 0, 2)],
+            9: [("k", 1, 0)],
+            10: [("k", 0, 3), ("q", 0, 3)],
+            11: [("k", 1, 1)],
+            12: [("k", 1, 2)],
+            13: [("k", 1, 3)],
+            14: [("q", 1, 3)],
+            18: [("q", 1, 2)],
+            22: [("q", 1, 1)],
+            26: [("q", 1, 0)],
+        }
+        jobs = []
+        jobs_of = {}
+        for x in range(NX):
+            h, t = seq[x]
+            state[x] = {"h": h, "t": t, "i": t // 4, "j": t % 4}
+            mine = []
+            for (kind, hh, grp) in prep_before.get(x, []):
+                mine.append(len(jobs))
+                jobs.append(prep_job(kind, hh, grp))
+            for b in range(t // 4 + 1):
+                mine.append(len(jobs))
+                jobs.append(qk_job(x, h, t, b))
+            jobs_of[x] = mine
+
+        def v_regroup(h):
+            if VREG_G and h == 1:
+                nc.gpsimd.tensor_scalar(
+                    out=v_grp[h][:], in0=v_sb[h][:].rearrange("p (g t) d -> p g d t", t=4),
+                    scalar1=1.0, scalar2=0.0, op0=ALU.mult, op1=ALU.add,
+                )
+            else:
+                nc.vector.tensor_copy(out=v_grp[h][:], in_=v_sb[h][:].rearrange("p (g t) d -> p g d t", t=4))
+
+        def v_quant(h):
+            nc.vector.quantize_mx(
+                out=v_codes[h][:].bitcast(FP8X4), scales=v_scales[h][:],
+                in_=v_grp[h][:].rearrange("p g d t -> p (g d t)"),
+            )
+
+        def exp_stage(x):
+            st = state[x]
+            n = P * (st["t"] + 1)
+            c0 = S - PASS * (st["i"] + 1)
+            st["c0"] = c0
+            rowsum = small.tile([P, 1], F32, name="rowsum")
+            st["rowsum"] = rowsum
+            nc.scalar.activation(
+                out=e_cls[4 * st["h"] + st["j"]][:, c0:c0 + n], in_=st["sneg"][:, 0:n], func=ACT.Exp,
+                bias=st["negm"], scale=-1.0, accum_out=rowsum[:],
+            )
+
+        def transpose_stage(x):
+            st = state[x]
+            npass = st["i"] + 1
+            ng = max(0, npass - G_KEEP)
+            st["ng"] = ng
+            e = e_cls[4 * st["h"] + st["j"]]
+            grouped = grp_pool.tile([P, 4 - 0, P, 4], BF16, name="grouped", align_bytes=64)
+            st["grouped"] = grouped
+            later = []
+            if ng > 0:
+                planes = plane_pool.tile([P, 3, 4, P], BF16, name="planes")
+                st["planes"] = planes
+            for g0 in range(0, npass, 2):
+                n2 = min(2, npass - g0)
+                xt = psum_x.tile([P, 2, 4, P], BF16, name="xt")
+                for g in range(g0, g0 + n2):
+                    for c in range(4):
+                        col = st["c0"] + PASS * g
+                        nc.tensor.transpose(out=xt[:, g - g0, c, :], in_=e[:, col + c:col + PASS:4], identity=ident[:])
+                nplain = max(0, min(g0 + n2, ng) - g0)
+                if nplain > 0:
+                    nc.scalar.copy(out=planes[:, g0:g0 + nplain, :, :], in_=xt[:, 0:nplain, :, :])
+                if nplain < n2:
+                    dst = grouped[:, g0 + nplain - ng:g0 + n2 - ng, :, :]
+                    src = xt[:, nplain:n2, :, :].rearrange("p g c x -> p g x c")
+                    if st["h"] == 1 and V_DIRECT_MOD > 0 and st["t"] % V_DIRECT_MOD == 0:
+                        later.append((dst, src))
+                    else:
+                        nc.scalar.copy(out=dst, in_=src)
+            return later
+
+        def gpsimd_stage(x):
+            st = state[x]
+            ng = st["ng"]
+            if ng > 0:
+                gg = gg_pool.tile([P, 3, P, 4], BF16, name="gg", align_bytes=64)
+                st["gg"] = gg
+                nc.gpsimd.tensor_scalar(
+                    out=gg[:, 0:ng, :, :], in0=st["planes"][:, 0:ng, :, :].rearrange("p g c x -> p g x c"),
+                    scalar1=1.0, scalar2=0.0, op0=ALU.mult, op1=ALU.add,
+                )
+
+        def quant_stage(x):
+            st = state[x]
+            npass = st["i"] + 1
+            ng = st["ng"]
+            codes = code_pool.tile([P, 4 * P], U32, name="codes", align_bytes=64)
+            scales = code_pool.tile([P, 4 * P], U8, name="scales", align_bytes=64)
+            st["codes"] = codes
+            st["scales"] = scales
+            widths = {0: [], 1: [1], 2: [2], 3: [2, 1], 4: [4]}
+            if ng > 0:
+                flat = st["gg"][:].rearrange("p g x c -> p (g x c)")
+                a = 0
+                for wd in widths[ng]:
+                    nc.vector.quantize_mx(
+                        out=codes[:, P * a:P * (a + wd)].bitcast(FP8X4), scales=scales[:, P * a:P * (a + wd)],
+                        in_=flat[:, PASS * a:PASS * (a + wd)],
+                    )
+                    a += wd
+            flat = st["grouped"][:].rearrange("p g x c -> p (g x c)")
+            a = 0
+            for wd in widths[npass - ng]:
+                nc.vector.quantize_mx(
+                    out=codes[:, P * (ng + a):P * (ng + a + wd)].bitcast(FP8X4), scales=scales[:, P * (ng + a):P * (ng + a + wd)],
+                    in_=flat[:, PASS * a:PASS * (a + wd)],
+                )
+                a += wd
+            recip = small.tile([P, 1], F32, name="recip")
+            st["recip"] = recip
+            nc.vector.reciprocal(out=recip[:], in_=st["rowsum"][:])
+
+        def pv_stage(x):
+            st = state[x]
+            npass = st["i"] + 1
+            h = st["h"]
+            pv = psum_o.tile([P, D], F32, name="pv")
+            st["pv"] = pv
+            for g in range(npass):
+                cols = slice(P * g, P * (g + 1))
+                nc.tensor.matmul_mx(
+                    out=pv[:], lhsT=st["codes"][:, cols].bitcast(FP8X4), lhsT_scale=st["scales"][:, cols],
+                    rhs=v_codes[h][:, cols].bitcast(FP8X4), rhs_scale=v_scales[h][:, cols],
+                    start=(g == 0), stop=(g == npass - 1),
+                )
+
+        def out_stage(x):
+            st = state[x]
+            o_sb = out_pool.tile([P, D], F32, name="o_sb")
+            nc.vector.tensor_scalar(out=o_sb[:], in0=st["pv"][:], scalar1=st["recip"][:, 0:1], scalar2=None, op0=ALU.mult)
+            nc.sync.dma_start(out=out_v[st["h"]][st["t"]], in_=o_sb[:])
+
+        for kind in ("k", "q"):
+            pe, ve = prep_job(kind, 0, 0)
+            pe()
+            ve()
+        issued = 0
+        done = 0
+        while issued < min(LOOKAHEAD, len(jobs)):
+            jobs[issued][0]()
+            issued += 1
+
+        def run_jobs(x, later):
+            cnt = 0
+            res = [issued, done]
+            for jb in jobs_of[x]:
+                assert jb == res[1]
+                jobs[jb][1]()
+                res[1] += 1
+                if res[0] < len(jobs):
+                    jobs[res[0]][0]()
+                    res[0] += 1
+                cnt += 1
+                if cnt == 2:
+                    for (dst, src) in later:
+                        nc.vector.tensor_copy(out=dst, in_=src)
+                    later = []
+            for (dst, src) in later:
+                nc.vector.tensor_copy(out=dst, in_=src)
+            return res
+
+        for x in range(AHEAD):
+            issued, done = run_jobs(x, [])
+        for x in range(NX + BEHIND + OUT_LAG):
+            if 0 <= x - BEHIND < NX:
+                quant_stage(x - BEHIND)
+            if 0 <= x - 2 < NX:
+                gpsimd_stage(x - 2)
+            if x < NX:
+                exp_stage(x)
+            later = []
+            if 0 <= x - 1 < NX:
+                later = transpose_stage(x - 1)
+            if 0 <= x - BEHIND < NX:
+                pv_stage(x - BEHIND)
+            if x + AHEAD < NX:
+                issued, done = run_jobs(x + AHEAD, later)
+            else:
+                for (dst, src) in later:
+                    nc.vector.tensor_copy(out=dst, in_=src)
+            if x == 0:
+                v_regroup(0)
+            if x == 1:
+                v_quant(0)
+            if x == 11:
+                v_regroup(1)
+            if x == 12:
+                v_quant(1)
+            if 0 <= x - BEHIND - OUT_LAG < NX:
+                out_stage(x - BEHIND - OUT_LAG)

@@ -18,27 +18,17 @@ S = 2048
 D = 128
 NT = S // P
 PASS = 512
+HALF = PASS // 2
+SH = S // 2
 SCALE = 1.0 / (D ** 0.5)
 MASK_VALUE = -1.0e30
 FLOPS = 4 * H * D * sum(PASS * PASS * (i + 1) for i in range(S // PASS))
 
-MANUAL = True
 LOOKAHEAD = 3
 S_BANKS = 4
 XT_BANKS = 2
 PV_BANKS = 2
-V_COPY_NPASS = 1
-OUT_LAG = 1
-PLANE_BUFS = 2
-GG_BUFS = 1
-G_KEEP = 1
-PREP_ON_S = 0
-V_DIRECT_MOD = 0
-VREG_G = 0
 AHEAD = 2
-BEHIND = 3
-SNEG_BUFS = 4
-GRP_BUFS = 4
 
 
 def tile_scaleddotproductattention_kernel(tc, q, k, v, is_causal, out):
@@ -50,13 +40,10 @@ def tile_scaleddotproductattention_kernel(tc, q, k, v, is_causal, out):
     out_v = out.rearrange("b h (c p) d -> (b h) c p d", p=P)
 
     with ExitStack() as ctx:
-        if MANUAL:
-            ctx.enter_context(tc.manual_schedule())
+        ctx.enter_context(tc.manual_schedule())
         keep = ctx.enter_context(tc.tile_pool(name="keep", bufs=1))
-        sneg_pool = ctx.enter_context(tc.tile_pool(name="sneg", bufs=SNEG_BUFS))
-        grp_pool = ctx.enter_context(tc.tile_pool(name="grp", bufs=GRP_BUFS))
-        plane_pool = ctx.enter_context(tc.tile_pool(name="plane", bufs=PLANE_BUFS))
-        gg_pool = ctx.enter_context(tc.tile_pool(name="gg", bufs=GG_BUFS))
+        sneg_pool = ctx.enter_context(tc.tile_pool(name="sneg", bufs=4))
+        grp_pool = ctx.enter_context(tc.tile_pool(name="grp", bufs=3))
         code_pool = ctx.enter_context(tc.tile_pool(name="code", bufs=3))
         small = ctx.enter_context(tc.tile_pool(name="small", bufs=8))
         out_pool = ctx.enter_context(tc.tile_pool(name="outp", bufs=4))
@@ -66,39 +53,44 @@ def tile_scaleddotproductattention_kernel(tc, q, k, v, is_causal, out):
 
         q_sb = [keep.tile([P, NT, D], BF16, name="q_sb%d" % h) for h in range(H)]
         k_sb = [keep.tile([P, NT, D], BF16, name="k_sb%d" % h) for h in range(H)]
-        v_sb = [keep.tile([P, NT, D], BF16, name="v_sb%d" % h) for h in range(H)]
+        v_sb = [keep.tile([P, 4, 4 * D], BF16, name="v_sb%d" % h) for h in range(H)]
         nc.sync.dma_start(out=k_sb[0][:, 0:4, :], in_=k_v[0][:, 0:4, :])
         nc.sync.dma_start(out=q_sb[0][:, 0:4, :], in_=q_v[0][:, 0:4, :])
         nc.sync.dma_start(out=k_sb[0][:, 4:8, :], in_=k_v[0][:, 4:8, :])
         nc.sync.dma_start(out=q_sb[0][:, 4:8, :], in_=q_v[0][:, 4:8, :])
-        nc.sync.dma_start(out=v_sb[0][:].rearrange("p (g t) d -> p g (t d)", t=4), in_=v_v[0])
+        nc.sync.dma_start(out=v_sb[0][:], in_=v_v[0])
         nc.sync.dma_start(out=k_sb[0][:, 8:NT, :], in_=k_v[0][:, 8:NT, :])
         nc.sync.dma_start(out=q_sb[0][:, 8:NT, :], in_=q_v[0][:, 8:NT, :])
         nc.sync.dma_start(out=k_sb[1][:], in_=k_v[1])
         nc.sync.dma_start(out=q_sb[1][:], in_=q_v[1])
-        nc.sync.dma_start(out=v_sb[1][:].rearrange("p (g t) d -> p g (t d)", t=4), in_=v_v[1])
+        nc.sync.dma_start(out=v_sb[1][:], in_=v_v[1])
 
         ident = keep.tile([P, P], BF16, name="ident")
         masks.make_identity(nc, ident[:])
+        ident_f = keep.tile([P, P], F32, name="ident_f")
+        masks.make_identity(nc, ident_f[:])
         mask_f = keep.tile([P, P], F32, name="mask_f")
         nc.gpsimd.memset(mask_f[:], 0.0)
         nc.gpsimd.affine_select(
             out=mask_f[:], in_=mask_f[:], compare_op=ALU.is_ge, fill=MASK_VALUE,
             base=0, pattern=[[-1, P]], channel_multiplier=1,
         )
-        mask_b = keep.tile([P, P], BF16, name="mask_b")
-        nc.vector.tensor_copy(out=mask_b[:], in_=mask_f[:])
+        mask_b = keep.tile([P, 2, P // 2], BF16, name="mask_b")
+        nc.vector.tensor_copy(
+            out=mask_b[:].rearrange("p u (a e) -> p u a e", e=2),
+            in_=mask_f[:].rearrange("p (a u e) -> p u a e", u=2, e=2),
+        )
         warm = keep.tile([P, 1], F32, name="warm")
         nc.vector.memset(warm[:], 0.0)
         warm2 = keep.tile([P, 1], F32, name="warm2")
         nc.scalar.activation(out=warm2[:], in_=warm[:], func=ACT.Exp)
-        e_cls = [keep.tile([P, S], BF16, name="e_cls%d" % c) for c in range(4 * H)]
+        e_cls = [keep.tile([P, 2, SH], BF16, name="e_cls%d" % c) for c in range(4 * H)]
         for c in range(4 * H):
             if c % 4 < 3:
-                nc.gpsimd.memset(e_cls[c][:, S - P * (3 - c % 4):S], 0.0)
+                nc.gpsimd.memset(e_cls[c][:, :, SH - 64 * (3 - c % 4):SH], 0.0)
 
         q_t = [keep.tile([P, S], BF16, name="q_t%d" % h) for h in range(H)]
-        k_t = [keep.tile([P, S], BF16, name="k_t%d" % h) for h in range(H)]
+        k_t = [keep.tile([P, 2, SH], BF16, name="k_t%d" % h) for h in range(H)]
         v_grp = [keep.tile([P, 4, D, 4], BF16, name="v_grp%d" % h, align_bytes=64) for h in range(H)]
         v_codes = [keep.tile([P, 4 * D], U32, name="v_codes%d" % h, align_bytes=64) for h in range(H)]
         v_scales = [keep.tile([P, 4 * D], U8, name="v_scales%d" % h, align_bytes=64) for h in range(H)]
@@ -108,7 +100,6 @@ def tile_scaleddotproductattention_kernel(tc, q, k, v, is_causal, out):
 
         def prep_job(kind, h, grp):
             src = (k_sb if kind == "k" else q_sb)[h]
-            dst = (k_t if kind == "k" else q_t)[h]
             box = {}
 
             def pe():
@@ -118,41 +109,47 @@ def tile_scaleddotproductattention_kernel(tc, q, k, v, is_causal, out):
                     nc.tensor.transpose(out=ps[:, c, :], in_=src[:, 4 * grp + c, :], identity=ident[:])
 
             def ve():
-                eng_copy = nc.scalar.copy if (PREP_ON_S and not (h == 0 and grp == 0)) else nc.vector.tensor_copy
-                eng_copy(
-                    out=dst[:, PASS * grp:PASS * (grp + 1)],
-                    in_=box["ps"][:].rearrange("p c x -> p (c x)"),
-                )
+                flat = box["ps"][:].rearrange("p c x -> p (c x)")
+                if kind == "k":
+                    nc.vector.tensor_copy(
+                        out=k_t[h][:, :, HALF * grp:HALF * (grp + 1)].bitcast(F32),
+                        in_=flat.bitcast(F32).rearrange("p (a u) -> p u a", u=2),
+                    )
+                else:
+                    nc.vector.tensor_copy(out=q_t[h][:, PASS * grp:PASS * (grp + 1)], in_=flat)
                 ready.add((kind, h, grp))
 
             return (pe, ve)
 
         def qk_job(x, h, t, b):
             i = t // 4
-            n = P * (t + 1)
-            w = min(PASS, n - PASS * b)
+            j = t % 4
+            hw = HALF if b < i else 64 * (j + 1)
             box = {}
 
             def pe():
                 assert ("q", h, i) in ready and all(("k", h, g) in ready for g in range(b + 1))
                 ps = psum_s.tile([P, PASS], F32, name="s_ps", tag="s")
-                box["ps"] = ps
+                view = ps[:, 0:2 * hw].rearrange("p (u n) -> p u n", u=2)
+                box["view"] = view
                 q_cols = q_t[h][:, P * t:P * (t + 1)]
+                k0 = HALF * b
                 if b < i:
-                    nc.tensor.matmul(out=ps[:, :], lhsT=q_cols, rhs=k_t[h][:, PASS * b:PASS * (b + 1)], start=True, stop=True)
+                    nc.tensor.matmul(out=view, lhsT=q_cols, rhs=k_t[h][:, :, k0:k0 + HALF], start=True, stop=True)
                 else:
-                    if w > P:
-                        nc.tensor.matmul(out=ps[:, 0:w - P], lhsT=q_cols, rhs=k_t[h][:, PASS * b:PASS * b + w - P], start=True, stop=True)
-                    nc.tensor.matmul(out=ps[:, w - P:w], lhsT=q_cols, rhs=k_t[h][:, n - P:n], start=True, stop=False)
-                    nc.tensor.matmul(out=ps[:, w - P:w], lhsT=ident[:], rhs=mask_b[:], start=False, stop=True)
+                    d0 = 64 * j
+                    if j > 0:
+                        nc.tensor.matmul(out=view[:, :, 0:d0], lhsT=q_cols, rhs=k_t[h][:, :, k0:k0 + d0], start=True, stop=True)
+                    nc.tensor.matmul(out=view[:, :, d0:d0 + 64], lhsT=q_cols, rhs=k_t[h][:, :, k0 + d0:k0 + d0 + 64], start=True, stop=False)
+                    nc.tensor.matmul(out=view[:, :, d0:d0 + 64], lhsT=ident[:], rhs=mask_b[:], start=False, stop=True)
 
             def ve():
                 st = state[x]
                 if b == 0:
-                    st["sneg"] = sneg_pool.tile([P, S], F32, name="sneg")
+                    st["sneg"] = sneg_pool.tile([P, 2, SH], F32, name="sneg")
                     st["pm"] = small.tile([P, 4], F32, name="pm")
                 nc.vector.tensor_scalar(
-                    out=st["sneg"][:, PASS * b:PASS * b + w], in0=box["ps"][:, 0:w],
+                    out=st["sneg"][:, :, HALF * b:HALF * b + hw], in0=box["view"],
                     scalar1=-SCALE, scalar2=None, op0=ALU.mult, op1=ALU.min,
                     accum_out=st["pm"][:, b:b + 1],
                 )
@@ -196,13 +193,7 @@ def tile_scaleddotproductattention_kernel(tc, q, k, v, is_causal, out):
             jobs_of[x] = mine
 
         def v_regroup(h):
-            if VREG_G and h == 1:
-                nc.gpsimd.tensor_scalar(
-                    out=v_grp[h][:], in0=v_sb[h][:].rearrange("p (g t) d -> p g d t", t=4),
-                    scalar1=1.0, scalar2=0.0, op0=ALU.mult, op1=ALU.add,
-                )
-            else:
-                nc.vector.tensor_copy(out=v_grp[h][:], in_=v_sb[h][:].rearrange("p (g t) d -> p g d t", t=4))
+            nc.vector.tensor_copy(out=v_grp[h][:], in_=v_sb[h][:].rearrange("p g (t d) -> p g d t", t=4))
 
         def v_quant(h):
             nc.vector.quantize_mx(
@@ -212,81 +203,43 @@ def tile_scaleddotproductattention_kernel(tc, q, k, v, is_causal, out):
 
         def exp_stage(x):
             st = state[x]
-            n = P * (st["t"] + 1)
-            c0 = S - PASS * (st["i"] + 1)
+            n = HALF * st["i"] + 64 * (st["j"] + 1)
+            c0 = SH - HALF * (st["i"] + 1)
             st["c0"] = c0
             rowsum = small.tile([P, 1], F32, name="rowsum")
             st["rowsum"] = rowsum
             nc.scalar.activation(
-                out=e_cls[4 * st["h"] + st["j"]][:, c0:c0 + n], in_=st["sneg"][:, 0:n], func=ACT.Exp,
+                out=e_cls[4 * st["h"] + st["j"]][:, :, c0:c0 + n], in_=st["sneg"][:, :, 0:n], func=ACT.Exp,
                 bias=st["negm"], scale=-1.0, accum_out=rowsum[:],
             )
 
         def transpose_stage(x):
             st = state[x]
             npass = st["i"] + 1
-            ng = max(0, npass - G_KEEP)
-            st["ng"] = ng
             e = e_cls[4 * st["h"] + st["j"]]
-            grouped = grp_pool.tile([P, 4 - 0, P, 4], BF16, name="grouped", align_bytes=64)
+            grouped = grp_pool.tile([P, 4, P, 2], F32, name="grouped", align_bytes=64)
             st["grouped"] = grouped
-            later = []
-            if ng > 0:
-                planes = plane_pool.tile([P, 3, 4, P], BF16, name="planes")
-                st["planes"] = planes
             for g0 in range(0, npass, 2):
                 n2 = min(2, npass - g0)
-                xt = psum_x.tile([P, 2, 4, P], BF16, name="xt")
+                xt = psum_x.tile([P, 2, 2, P], F32, name="xt")
                 for g in range(g0, g0 + n2):
-                    for c in range(4):
-                        col = st["c0"] + PASS * g
-                        nc.tensor.transpose(out=xt[:, g - g0, c, :], in_=e[:, col + c:col + PASS:4], identity=ident[:])
-                nplain = max(0, min(g0 + n2, ng) - g0)
-                if nplain > 0:
-                    nc.scalar.copy(out=planes[:, g0:g0 + nplain, :, :], in_=xt[:, 0:nplain, :, :])
-                if nplain < n2:
-                    dst = grouped[:, g0 + nplain - ng:g0 + n2 - ng, :, :]
-                    src = xt[:, nplain:n2, :, :].rearrange("p g c x -> p g x c")
-                    if st["h"] == 1 and V_DIRECT_MOD > 0 and st["t"] % V_DIRECT_MOD == 0:
-                        later.append((dst, src))
-                    else:
-                        nc.scalar.copy(out=dst, in_=src)
-            return later
-
-        def gpsimd_stage(x):
-            st = state[x]
-            ng = st["ng"]
-            if ng > 0:
-                gg = gg_pool.tile([P, 3, P, 4], BF16, name="gg", align_bytes=64)
-                st["gg"] = gg
-                nc.gpsimd.tensor_scalar(
-                    out=gg[:, 0:ng, :, :], in0=st["planes"][:, 0:ng, :, :].rearrange("p g c x -> p g x c"),
-                    scalar1=1.0, scalar2=0.0, op0=ALU.mult, op1=ALU.add,
-                )
+                    for u in range(2):
+                        col = st["c0"] + HALF * g
+                        nc.tensor.transpose(out=xt[:, g - g0, u, :], in_=e[:, u, col:col + HALF].bitcast(F32), identity=ident_f[:])
+                nc.scalar.copy(out=grouped[:, g0:g0 + n2, :, :], in_=xt[:, 0:n2, :, :].rearrange("p g u x -> p g x u"))
 
         def quant_stage(x):
             st = state[x]
             npass = st["i"] + 1
-            ng = st["ng"]
             codes = code_pool.tile([P, 4 * P], U32, name="codes", align_bytes=64)
             scales = code_pool.tile([P, 4 * P], U8, name="scales", align_bytes=64)
             st["codes"] = codes
             st["scales"] = scales
-            widths = {0: [], 1: [1], 2: [2], 3: [2, 1], 4: [4]}
-            if ng > 0:
-                flat = st["gg"][:].rearrange("p g x c -> p (g x c)")
-                a = 0
-                for wd in widths[ng]:
-                    nc.vector.quantize_mx(
-                        out=codes[:, P * a:P * (a + wd)].bitcast(FP8X4), scales=scales[:, P * a:P * (a + wd)],
-                        in_=flat[:, PASS * a:PASS * (a + wd)],
-                    )
-                    a += wd
-            flat = st["grouped"][:].rearrange("p g x c -> p (g x c)")
+            flat = st["grouped"][:].rearrange("p g x u -> p (g x u)").bitcast(BF16)
             a = 0
-            for wd in widths[npass - ng]:
+            for wd in {1: [1], 2: [2], 3: [2, 1], 4: [4]}[npass]:
                 nc.vector.quantize_mx(
-                    out=codes[:, P * (ng + a):P * (ng + a + wd)].bitcast(FP8X4), scales=scales[:, P * (ng + a):P * (ng + a + wd)],
+                    out=codes[:, P * a:P * (a + wd)].bitcast(FP8X4), scales=scales[:, P * a:P * (a + wd)],
                     in_=flat[:, PASS * a:PASS * (a + wd)],
                 )
                 a += wd
@@ -324,8 +277,7 @@ def tile_scaleddotproductattention_kernel(tc, q, k, v, is_causal, out):
             jobs[issued][0]()
             issued += 1
 
-        def run_jobs(x, later):
-            cnt = 0
+        def run_jobs(x):
             res = [issued, done]
             for jb in jobs_of[x]:
                 assert jb == res[1]
@@ -334,34 +286,21 @@ def tile_scaleddotproductattention_kernel(tc, q, k, v, is_causal, out):
                 if res[0] < len(jobs):
                     jobs[res[0]][0]()
                     res[0] += 1
-                cnt += 1
-                if cnt == 2:
-                    for (dst, src) in later:
-                        nc.vector.tensor_copy(out=dst, in_=src)
-                    later = []
-            for (dst, src) in later:
-                nc.vector.tensor_copy(out=dst, in_=src)
             return res
 
         for x in range(AHEAD):
-            issued, done = run_jobs(x, [])
-        for x in range(NX + BEHIND + OUT_LAG):
-            if 0 <= x - BEHIND < NX:
-                quant_stage(x - BEHIND)
+            issued, done = run_jobs(x)
+        for x in range(NX + 3):
             if 0 <= x - 2 < NX:
-                gpsimd_stage(x - 2)
+                quant_stage(x - 2)
             if x < NX:
                 exp_stage(x)
-            later = []
             if 0 <= x - 1 < NX:
-                later = transpose_stage(x - 1)
-            if 0 <= x - BEHIND < NX:
-                pv_stage(x - BEHIND)
+                transpose_stage(x - 1)
+            if 0 <= x - 2 < NX:
+                pv_stage(x - 2)
             if x + AHEAD < NX:
-                issued, done = run_jobs(x + AHEAD, later)
-            else:
-                for (dst, src) in later:
-                    nc.vector.tensor_copy(out=dst, in_=src)
+                issued, done = run_jobs(x + AHEAD)
             if x == 0:
                 v_regroup(0)
             if x == 1:
@@ -370,5 +309,5 @@ def tile_scaleddotproductattention_kernel(tc, q, k, v, is_causal, out):
                 v_regroup(1)
             if x == 12:
                 v_quant(1)
-            if 0 <= x - BEHIND - OUT_LAG < NX:
-                out_stage(x - BEHIND - OUT_LAG)
+            if 0 <= x - 3 < NX:
+                out_stage(x - 3)

@@ -25,6 +25,7 @@ MASK_VALUE = -1.0e30
 FLOPS = 4 * H * D * sum(PASS * PASS * (i + 1) for i in range(S // PASS))
 
 LOOKAHEAD = 3
+V_STEPS = {0: (0, 0), 4: (0, 1), 10: (1, 1), 12: (1, 0)}
 S_BANKS = 4
 XT_BANKS = 2
 PV_BANKS = 2
@@ -56,9 +57,10 @@ def tile_scaleddotproductattention_kernel(tc, q, k, v, is_causal, out):
         v_sb = [keep.tile([P, 4, 4 * D], BF16, name="v_sb%d" % h) for h in range(H)]
         nc.sync.dma_start(out=k_sb[0][:, 0:4, :], in_=k_v[0][:, 0:4, :])
         nc.sync.dma_start(out=q_sb[0][:, 0:4, :], in_=q_v[0][:, 0:4, :])
+        nc.sync.dma_start(out=v_sb[0][:, 0:2, :], in_=v_v[0][:, 0:2, :])
         nc.sync.dma_start(out=k_sb[0][:, 4:8, :], in_=k_v[0][:, 4:8, :])
         nc.sync.dma_start(out=q_sb[0][:, 4:8, :], in_=q_v[0][:, 4:8, :])
-        nc.sync.dma_start(out=v_sb[0][:], in_=v_v[0])
+        nc.sync.dma_start(out=v_sb[0][:, 2:4, :], in_=v_v[0][:, 2:4, :])
         nc.sync.dma_start(out=k_sb[0][:, 8:NT, :], in_=k_v[0][:, 8:NT, :])
         nc.sync.dma_start(out=q_sb[0][:, 8:NT, :], in_=q_v[0][:, 8:NT, :])
         nc.sync.dma_start(out=k_sb[1][:], in_=k_v[1])
@@ -67,14 +69,14 @@ def tile_scaleddotproductattention_kernel(tc, q, k, v, is_causal, out):
 
         ident = keep.tile([P, P], BF16, name="ident")
         masks.make_identity(nc, ident[:])
-        ident_f = keep.tile([P, P], F32, name="ident_f")
-        masks.make_identity(nc, ident_f[:])
         mask_f = keep.tile([P, P], F32, name="mask_f")
         nc.gpsimd.memset(mask_f[:], 0.0)
         nc.gpsimd.affine_select(
             out=mask_f[:], in_=mask_f[:], compare_op=ALU.is_ge, fill=MASK_VALUE,
             base=0, pattern=[[-1, P]], channel_multiplier=1,
         )
+        ident_f = keep.tile([P, P], F32, name="ident_f")
+        masks.make_identity(nc, ident_f[:])
         mask_b = keep.tile([P, 2, P // 2], BF16, name="mask_b")
         nc.vector.tensor_copy(
             out=mask_b[:].rearrange("p u (a e) -> p u a e", e=2),
@@ -109,14 +111,15 @@ def tile_scaleddotproductattention_kernel(tc, q, k, v, is_causal, out):
                     nc.tensor.transpose(out=ps[:, c, :], in_=src[:, 4 * grp + c, :], identity=ident[:])
 
             def ve():
-                flat = box["ps"][:].rearrange("p c x -> p (c x)")
+                words = box["ps"][:].rearrange("p c x -> p (c x)").bitcast(F32)
+                copy = nc.vector.tensor_copy if (kind, h, grp) == ("k", 0, 0) else nc.scalar.copy
                 if kind == "k":
-                    nc.vector.tensor_copy(
+                    copy(
                         out=k_t[h][:, :, HALF * grp:HALF * (grp + 1)].bitcast(F32),
-                        in_=flat.bitcast(F32).rearrange("p (a u) -> p u a", u=2),
+                        in_=words.rearrange("p (a u) -> p u a", u=2),
                     )
                 else:
-                    nc.vector.tensor_copy(out=q_t[h][:, PASS * grp:PASS * (grp + 1)], in_=flat)
+                    copy(out=q_t[h][:, PASS * grp:PASS * (grp + 1)].bitcast(F32), in_=words)
                 ready.add((kind, h, grp))
 
             return (pe, ve)
@@ -156,7 +159,15 @@ def tile_scaleddotproductattention_kernel(tc, q, k, v, is_causal, out):
                 if b == i:
                     if i > 0:
                         negm = small.tile([P, 1], F32, name="negm")
-                        nc.vector.tensor_reduce(out=negm[:], in_=st["pm"][:, 0:i + 1], axis=AX.X, op=ALU.min)
+                        pm = st["pm"]
+                        if i == 1:
+                            nc.gpsimd.tensor_scalar(out=negm[:], in0=pm[:, 0:1], scalar1=pm[:, 1:2], scalar2=None, op0=ALU.min)
+                        else:
+                            nc.gpsimd.tensor_scalar(out=negm[:], in0=pm[:, 0:1], scalar1=pm[:, 1:2], scalar2=pm[:, 2:3], op0=ALU.min, op1=ALU.min)
+                        if i == 3:
+                            negm3 = small.tile([P, 1], F32, name="negm3")
+                            nc.gpsimd.tensor_scalar(out=negm3[:], in0=negm[:], scalar1=pm[:, 3:4], scalar2=None, op0=ALU.min)
+                            negm = negm3
                         st["negm"] = negm[:, 0:1]
                     else:
                         st["negm"] = st["pm"][:, 0:1]
@@ -192,13 +203,18 @@ def tile_scaleddotproductattention_kernel(tc, q, k, v, is_causal, out):
                 jobs.append(qk_job(x, h, t, b))
             jobs_of[x] = mine
 
-        def v_regroup(h):
-            nc.vector.tensor_copy(out=v_grp[h][:], in_=v_sb[h][:].rearrange("p g (t d) -> p g d t", t=4))
+        def v_regroup(h, half):
+            gs = slice(2 * half, 2 * half + 2)
+            nc.gpsimd.tensor_scalar(
+                out=v_grp[h][:, gs], in0=v_sb[h][:, gs, :].rearrange("p g (t d) -> p g d t", t=4),
+                scalar1=1.0, scalar2=0.0, op0=ALU.mult, op1=ALU.add,
+            )
 
-        def v_quant(h):
+        def v_quant(h, half):
+            cols = slice(2 * D * half, 2 * D * (half + 1))
             nc.vector.quantize_mx(
-                out=v_codes[h][:].bitcast(FP8X4), scales=v_scales[h][:],
-                in_=v_grp[h][:].rearrange("p g d t -> p (g d t)"),
+                out=v_codes[h][:, cols].bitcast(FP8X4), scales=v_scales[h][:, cols],
+                in_=v_grp[h][:, 2 * half:2 * half + 2].rearrange("p g d t -> p (g d t)"),
             )
 
         def exp_stage(x):
@@ -206,11 +222,13 @@ def tile_scaleddotproductattention_kernel(tc, q, k, v, is_causal, out):
             n = HALF * st["i"] + 64 * (st["j"] + 1)
             c0 = SH - HALF * (st["i"] + 1)
             st["c0"] = c0
-            rowsum = small.tile([P, 1], F32, name="rowsum")
-            st["rowsum"] = rowsum
+            if x % 2 == 0:
+                st["rowsum"] = small.tile([P, 2], F32, name="rowsum")
+            else:
+                st["rowsum"] = state[x - 1]["rowsum"]
             nc.scalar.activation(
                 out=e_cls[4 * st["h"] + st["j"]][:, :, c0:c0 + n], in_=st["sneg"][:, :, 0:n], func=ACT.Exp,
-                bias=st["negm"], scale=-1.0, accum_out=rowsum[:],
+                bias=st["negm"], scale=-1.0, accum_out=st["rowsum"][:, x % 2:x % 2 + 1],
             )
 
         def transpose_stage(x):
@@ -243,9 +261,11 @@ def tile_scaleddotproductattention_kernel(tc, q, k, v, is_causal, out):
                     in_=flat[:, PASS * a:PASS * (a + wd)],
                 )
                 a += wd
-            recip = small.tile([P, 1], F32, name="recip")
-            st["recip"] = recip
-            nc.vector.reciprocal(out=recip[:], in_=st["rowsum"][:])
+            if x % 2 == 1:
+                recip = small.tile([P, 2], F32, name="recip")
+                st["recip"] = recip[:, 1:2]
+                state[x - 1]["recip"] = recip[:, 0:1]
+                nc.vector.reciprocal(out=recip[:], in_=st["rowsum"][:])
 
         def pv_stage(x):
             st = state[x]
@@ -264,7 +284,7 @@ def tile_scaleddotproductattention_kernel(tc, q, k, v, is_causal, out):
         def out_stage(x):
             st = state[x]
             o_sb = out_pool.tile([P, D], F32, name="o_sb")
-            nc.vector.tensor_scalar(out=o_sb[:], in0=st["pv"][:], scalar1=st["recip"][:, 0:1], scalar2=None, op0=ALU.mult)
+            nc.vector.tensor_scalar(out=o_sb[:], in0=st["pv"][:], scalar1=st["recip"], scalar2=None, op0=ALU.mult)
             nc.sync.dma_start(out=out_v[st["h"]][st["t"]], in_=o_sb[:])
 
         for kind in ("k", "q"):
@@ -301,13 +321,9 @@ def tile_scaleddotproductattention_kernel(tc, q, k, v, is_causal, out):
                 pv_stage(x - 2)
             if x + AHEAD < NX:
                 issued, done = run_jobs(x + AHEAD)
-            if x == 0:
-                v_regroup(0)
-            if x == 1:
-                v_quant(0)
-            if x == 11:
-                v_regroup(1)
-            if x == 12:
-                v_quant(1)
+            if x in V_STEPS:
+                v_regroup(*V_STEPS[x])
+            if x - 1 in V_STEPS:
+                v_quant(*V_STEPS[x - 1])
             if 0 <= x - 3 < NX:
                 out_stage(x - 3)

@@ -24,12 +24,22 @@ SCALE = 1.0 / (D ** 0.5)
 MASK_VALUE = -1.0e30
 FLOPS = 4 * H * D * sum(PASS * PASS * (i + 1) for i in range(S // PASS))
 
-LOOKAHEAD = 3
-V_STEPS = {0: (0, 0), 4: (0, 1), 10: (1, 1), 12: (1, 0)}
-S_BANKS = 4
-XT_BANKS = 2
+S_BANKS = 3
+XT_BANKS = 3
 PV_BANKS = 2
-AHEAD = 2
+LOOKAHEAD = 3
+A = 2
+C = 1
+Q = 3
+O = 1
+TPOS = (0, 0)
+PPOS = 0
+QPOS = 0
+OPOS = 9
+OUT_S = 0
+VCOPY = ()
+V_STEPS = {0: (0, 0), 4: (0, 1), 10: (1, 1), 12: (1, 0)}
+PREP_AHEAD = 1
 
 
 def tile_scaleddotproductattention_kernel(tc, q, k, v, is_causal, out):
@@ -44,9 +54,9 @@ def tile_scaleddotproductattention_kernel(tc, q, k, v, is_causal, out):
         ctx.enter_context(tc.manual_schedule())
         keep = ctx.enter_context(tc.tile_pool(name="keep", bufs=1))
         sneg_pool = ctx.enter_context(tc.tile_pool(name="sneg", bufs=4))
-        grp_pool = ctx.enter_context(tc.tile_pool(name="grp", bufs=3))
+        grp_pool = ctx.enter_context(tc.tile_pool(name="grp", bufs=4))
         code_pool = ctx.enter_context(tc.tile_pool(name="code", bufs=3))
-        small = ctx.enter_context(tc.tile_pool(name="small", bufs=8))
+        small = ctx.enter_context(tc.tile_pool(name="small", bufs=12))
         out_pool = ctx.enter_context(tc.tile_pool(name="outp", bufs=4))
         psum_s = ctx.enter_context(tc.psum_pool(name="ps_s", bufs=S_BANKS))
         psum_x = ctx.enter_context(tc.psum_pool(name="ps_x", bufs=XT_BANKS))
@@ -105,7 +115,7 @@ def tile_scaleddotproductattention_kernel(tc, q, k, v, is_causal, out):
             box = {}
 
             def pe():
-                ps = psum_s.tile([P, 4, P], BF16, name="prep_ps", tag="s")
+                ps = psum_x.tile([P, 4, P], BF16, name="prep_ps", tag="x")
                 box["ps"] = ps
                 for c in range(4):
                     nc.tensor.transpose(out=ps[:, c, :], in_=src[:, 4 * grp + c, :], identity=ident[:])
@@ -176,31 +186,19 @@ def tile_scaleddotproductattention_kernel(tc, q, k, v, is_causal, out):
 
         seq = [(0, t) for t in range(NT)] + [(1, t) for t in range(NT - 1, -1, -1)]
         NX = len(seq)
-        prep_before = {
-            2: [("k", 0, 1), ("q", 0, 1)],
-            6: [("k", 0, 2), ("q", 0, 2)],
-            9: [("k", 1, 0)],
-            10: [("k", 0, 3), ("q", 0, 3)],
-            11: [("k", 1, 1)],
-            12: [("k", 1, 2)],
-            13: [("k", 1, 3)],
-            14: [("q", 1, 3)],
-            18: [("q", 1, 2)],
-            22: [("q", 1, 1)],
-            26: [("q", 1, 0)],
-        }
         jobs = []
+        needs = []
+        width = []
         jobs_of = {}
         for x in range(NX):
             h, t = seq[x]
             state[x] = {"h": h, "t": t, "i": t // 4, "j": t % 4}
             mine = []
-            for (kind, hh, grp) in prep_before.get(x, []):
-                mine.append(len(jobs))
-                jobs.append(prep_job(kind, hh, grp))
             for b in range(t // 4 + 1):
                 mine.append(len(jobs))
                 jobs.append(qk_job(x, h, t, b))
+                needs.append([("q", h, t // 4), ("k", h, b)])
+                width.append(t // 4 + 1)
             jobs_of[x] = mine
 
         def v_regroup(h, half):
@@ -231,20 +229,23 @@ def tile_scaleddotproductattention_kernel(tc, q, k, v, is_causal, out):
                 bias=st["negm"], scale=-1.0, accum_out=st["rowsum"][:, x % 2:x % 2 + 1],
             )
 
-        def transpose_stage(x):
+        def transpose_stage(x, half):
             st = state[x]
             npass = st["i"] + 1
             e = e_cls[4 * st["h"] + st["j"]]
-            grouped = grp_pool.tile([P, 4, P, 2], F32, name="grouped", align_bytes=64)
-            st["grouped"] = grouped
-            for g0 in range(0, npass, 2):
-                n2 = min(2, npass - g0)
-                xt = psum_x.tile([P, 2, 2, P], F32, name="xt")
-                for g in range(g0, g0 + n2):
-                    for u in range(2):
-                        col = st["c0"] + HALF * g
-                        nc.tensor.transpose(out=xt[:, g - g0, u, :], in_=e[:, u, col:col + HALF].bitcast(F32), identity=ident_f[:])
-                nc.scalar.copy(out=grouped[:, g0:g0 + n2, :, :], in_=xt[:, 0:n2, :, :].rearrange("p g u x -> p g x u"))
+            if half == 0:
+                st["grouped"] = grp_pool.tile([P, 4, P, 2], F32, name="grouped", align_bytes=64)
+            g0 = 2 * half
+            if g0 >= npass:
+                return
+            n2 = min(2, npass - g0)
+            xt = psum_x.tile([P, 2, 2, P], F32, name="xt", tag="x")
+            for g in range(g0, g0 + n2):
+                for u in range(2):
+                    col = st["c0"] + HALF * g
+                    nc.tensor.transpose(out=xt[:, g - g0, u, :], in_=e[:, u, col:col + HALF].bitcast(F32), identity=ident_f[:])
+            copy = nc.vector.tensor_copy if (st["t"], half) in VCOPY else nc.scalar.copy
+            copy(out=st["grouped"][:, g0:g0 + n2, :, :], in_=xt[:, 0:n2, :, :].rearrange("p g u x -> p g x u"))
 
         def quant_stage(x):
             st = state[x]
@@ -284,46 +285,59 @@ def tile_scaleddotproductattention_kernel(tc, q, k, v, is_causal, out):
         def out_stage(x):
             st = state[x]
             o_sb = out_pool.tile([P, D], F32, name="o_sb")
-            nc.vector.tensor_scalar(out=o_sb[:], in0=st["pv"][:], scalar1=st["recip"], scalar2=None, op0=ALU.mult)
+            if OUT_S and x % OUT_S == 0:
+                nc.scalar.activation(out=o_sb[:], in_=st["pv"][:], func=ACT.Copy, scale=st["recip"])
+            else:
+                nc.vector.tensor_scalar(out=o_sb[:], in0=st["pv"][:], scalar1=st["recip"], scalar2=None, op0=ALU.mult)
             nc.sync.dma_start(out=out_v[st["h"]][st["t"]], in_=o_sb[:])
 
         for kind in ("k", "q"):
             pe, ve = prep_job(kind, 0, 0)
             pe()
             ve()
-        issued = 0
-        done = 0
-        while issued < min(LOOKAHEAD, len(jobs)):
-            jobs[issued][0]()
-            issued += 1
+        count = {"issued": 0}
 
-        def run_jobs(x):
-            res = [issued, done]
-            for jb in jobs_of[x]:
-                assert jb == res[1]
+        def prepare(args):
+            pe, ve = prep_job(*args)
+            pe()
+            ve()
+
+        def issue(upto):
+            while count["issued"] < min(upto, len(jobs)):
+                n = count["issued"]
+                for args in needs[n]:
+                    if args not in ready:
+                        prepare(args)
+                ahead = [a for m in range(n, min(n + PREP_AHEAD * width[n] + 1, len(jobs))) for a in needs[m] if a not in ready]
+                if ahead:
+                    prepare(ahead[0])
+                jobs[n][0]()
+                count["issued"] += 1
+
+        for s in range(-A, NX + Q + O):
+            mine = jobs_of.get(s + A, [])
+
+            def at(pos, n):
+                last = pos == n
+                for half in range(2):
+                    if (TPOS[half] == pos or (last and TPOS[half] > n)) and 0 <= s - C < NX:
+                        transpose_stage(s - C, half)
+                if (QPOS == pos or (last and QPOS > n)) and 0 <= s - Q < NX:
+                    quant_stage(s - Q)
+                if (PPOS == pos or (last and PPOS > n)) and 0 <= s - Q < NX:
+                    pv_stage(s - Q)
+                if (OPOS == pos or (last and OPOS > n)) and 0 <= s - Q - O < NX:
+                    out_stage(s - Q - O)
+
+            if 0 <= s < NX:
+                exp_stage(s)
+            for n, jb in enumerate(mine):
+                at(n, len(mine))
+                issue(jb + 1)
                 jobs[jb][1]()
-                res[1] += 1
-                if res[0] < len(jobs):
-                    jobs[res[0]][0]()
-                    res[0] += 1
-            return res
-
-        for x in range(AHEAD):
-            issued, done = run_jobs(x)
-        for x in range(NX + 3):
-            if 0 <= x - 2 < NX:
-                quant_stage(x - 2)
-            if x < NX:
-                exp_stage(x)
-            if 0 <= x - 1 < NX:
-                transpose_stage(x - 1)
-            if 0 <= x - 2 < NX:
-                pv_stage(x - 2)
-            if x + AHEAD < NX:
-                issued, done = run_jobs(x + AHEAD)
-            if x in V_STEPS:
-                v_regroup(*V_STEPS[x])
-            if x - 1 in V_STEPS:
-                v_quant(*V_STEPS[x - 1])
-            if 0 <= x - 3 < NX:
-                out_stage(x - 3)
+                issue(jb + 1 + LOOKAHEAD)
+            at(len(mine), len(mine))
+            if s in V_STEPS:
+                v_regroup(*V_STEPS[s])
+            if s - 1 in V_STEPS:
+                v_quant(*V_STEPS[s - 1])

@@ -37,9 +37,14 @@ PPOS = 0
 QPOS = 0
 OPOS = 9
 OUT_S = 0
-VCOPY = ()
+VCOPY = tuple((1, i, j, 1) for i in (2, 3) for j in (0, 2))
 V_STEPS = {0: (0, 0), 4: (0, 1), 10: (1, 1), 12: (1, 0)}
 PREP_AHEAD = 1
+PREP_OFF = 0
+TL = 1
+FIRST = ((0, 1), (1, 4))
+PREP_V = ()
+VC_POS = 9
 
 
 def tile_scaleddotproductattention_kernel(tc, q, k, v, is_causal, out):
@@ -57,7 +62,7 @@ def tile_scaleddotproductattention_kernel(tc, q, k, v, is_causal, out):
         grp_pool = ctx.enter_context(tc.tile_pool(name="grp", bufs=4))
         code_pool = ctx.enter_context(tc.tile_pool(name="code", bufs=3))
         small = ctx.enter_context(tc.tile_pool(name="small", bufs=12))
-        out_pool = ctx.enter_context(tc.tile_pool(name="outp", bufs=4))
+        out_pool = ctx.enter_context(tc.tile_pool(name="outp", bufs=8))
         psum_s = ctx.enter_context(tc.psum_pool(name="ps_s", bufs=S_BANKS))
         psum_x = ctx.enter_context(tc.psum_pool(name="ps_x", bufs=XT_BANKS))
         psum_o = ctx.enter_context(tc.psum_pool(name="ps_o", bufs=PV_BANKS))
@@ -65,14 +70,17 @@ def tile_scaleddotproductattention_kernel(tc, q, k, v, is_causal, out):
         q_sb = [keep.tile([P, NT, D], BF16, name="q_sb%d" % h) for h in range(H)]
         k_sb = [keep.tile([P, NT, D], BF16, name="k_sb%d" % h) for h in range(H)]
         v_sb = [keep.tile([P, 4, 4 * D], BF16, name="v_sb%d" % h) for h in range(H)]
-        nc.sync.dma_start(out=k_sb[0][:, 0:4, :], in_=k_v[0][:, 0:4, :])
-        nc.sync.dma_start(out=q_sb[0][:, 0:4, :], in_=q_v[0][:, 0:4, :])
-        nc.sync.dma_start(out=v_sb[0][:, 0:2, :], in_=v_v[0][:, 0:2, :])
+        for lo, hi in FIRST:
+            nc.sync.dma_start(out=k_sb[0][:, lo:hi, :], in_=k_v[0][:, lo:hi, :])
+            nc.sync.dma_start(out=q_sb[0][:, lo:hi, :], in_=q_v[0][:, lo:hi, :])
         nc.sync.dma_start(out=k_sb[0][:, 4:8, :], in_=k_v[0][:, 4:8, :])
         nc.sync.dma_start(out=q_sb[0][:, 4:8, :], in_=q_v[0][:, 4:8, :])
+        nc.sync.dma_start(out=v_sb[0][:, 0:2, :], in_=v_v[0][:, 0:2, :])
+        nc.sync.dma_start(out=k_sb[0][:, 8:12, :], in_=k_v[0][:, 8:12, :])
+        nc.sync.dma_start(out=q_sb[0][:, 8:12, :], in_=q_v[0][:, 8:12, :])
         nc.sync.dma_start(out=v_sb[0][:, 2:4, :], in_=v_v[0][:, 2:4, :])
-        nc.sync.dma_start(out=k_sb[0][:, 8:NT, :], in_=k_v[0][:, 8:NT, :])
-        nc.sync.dma_start(out=q_sb[0][:, 8:NT, :], in_=q_v[0][:, 8:NT, :])
+        nc.sync.dma_start(out=k_sb[0][:, 12:NT, :], in_=k_v[0][:, 12:NT, :])
+        nc.sync.dma_start(out=q_sb[0][:, 12:NT, :], in_=q_v[0][:, 12:NT, :])
         nc.sync.dma_start(out=k_sb[1][:], in_=k_v[1])
         nc.sync.dma_start(out=q_sb[1][:], in_=q_v[1])
         nc.sync.dma_start(out=v_sb[1][:], in_=v_v[1])
@@ -110,26 +118,26 @@ def tile_scaleddotproductattention_kernel(tc, q, k, v, is_causal, out):
         ready = set()
         state = {}
 
-        def prep_job(kind, h, grp):
+        def prep_job(kind, h, grp, lo=0, hi=4):
             src = (k_sb if kind == "k" else q_sb)[h]
             box = {}
 
             def pe():
                 ps = psum_x.tile([P, 4, P], BF16, name="prep_ps", tag="x")
                 box["ps"] = ps
-                for c in range(4):
+                for c in range(lo, hi):
                     nc.tensor.transpose(out=ps[:, c, :], in_=src[:, 4 * grp + c, :], identity=ident[:])
 
             def ve():
-                words = box["ps"][:].rearrange("p c x -> p (c x)").bitcast(F32)
-                copy = nc.vector.tensor_copy if (kind, h, grp) == ("k", 0, 0) else nc.scalar.copy
+                words = box["ps"][:, lo:hi, :].rearrange("p c x -> p (c x)").bitcast(F32)
+                copy = nc.vector.tensor_copy if (kind, h, grp) == ("k", 0, 0) or (kind, h, grp) in PREP_V else nc.scalar.copy
                 if kind == "k":
                     copy(
-                        out=k_t[h][:, :, HALF * grp:HALF * (grp + 1)].bitcast(F32),
+                        out=k_t[h][:, :, HALF * grp + 64 * lo:HALF * grp + 64 * hi].bitcast(F32),
                         in_=words.rearrange("p (a u) -> p u a", u=2),
                     )
                 else:
-                    copy(out=q_t[h][:, PASS * grp:PASS * (grp + 1)].bitcast(F32), in_=words)
+                    copy(out=q_t[h][:, PASS * grp + P * lo:PASS * grp + P * hi].bitcast(F32), in_=words)
                 ready.add((kind, h, grp))
 
             return (pe, ve)
@@ -244,8 +252,12 @@ def tile_scaleddotproductattention_kernel(tc, q, k, v, is_causal, out):
                 for u in range(2):
                     col = st["c0"] + HALF * g
                     nc.tensor.transpose(out=xt[:, g - g0, u, :], in_=e[:, u, col:col + HALF].bitcast(F32), identity=ident_f[:])
-            copy = nc.vector.tensor_copy if (st["t"], half) in VCOPY else nc.scalar.copy
-            copy(out=st["grouped"][:, g0:g0 + n2, :, :], in_=xt[:, 0:n2, :, :].rearrange("p g u x -> p g x u"))
+            dst = st["grouped"][:, g0:g0 + n2, :, :]
+            src = xt[:, 0:n2, :, :].rearrange("p g u x -> p g x u")
+            if (st["h"], st["i"], st["j"], half) in VCOPY:
+                later.append((dst, src))
+            else:
+                nc.scalar.copy(out=dst, in_=src)
 
         def quant_stage(x):
             st = state[x]
@@ -285,14 +297,14 @@ def tile_scaleddotproductattention_kernel(tc, q, k, v, is_causal, out):
         def out_stage(x):
             st = state[x]
             o_sb = out_pool.tile([P, D], F32, name="o_sb")
-            if OUT_S and x % OUT_S == 0:
+            if OUT_S and st["h"] == 0 and x % OUT_S == 0:
                 nc.scalar.activation(out=o_sb[:], in_=st["pv"][:], func=ACT.Copy, scale=st["recip"])
             else:
                 nc.vector.tensor_scalar(out=o_sb[:], in0=st["pv"][:], scalar1=st["recip"], scalar2=None, op0=ALU.mult)
             nc.sync.dma_start(out=out_v[st["h"]][st["t"]], in_=o_sb[:])
 
-        for kind in ("k", "q"):
-            pe, ve = prep_job(kind, 0, 0)
+        first = [prep_job(kind, 0, 0, lo, hi) for (lo, hi) in FIRST for kind in ("k", "q")]
+        for pe, ve in first:
             pe()
             ve()
         count = {"issued": 0}
@@ -308,11 +320,22 @@ def tile_scaleddotproductattention_kernel(tc, q, k, v, is_causal, out):
                 for args in needs[n]:
                     if args not in ready:
                         prepare(args)
-                ahead = [a for m in range(n, min(n + PREP_AHEAD * width[n] + 1, len(jobs))) for a in needs[m] if a not in ready]
+                ahead = [a for m in range(n, min(n + max(0, PREP_AHEAD * width[n] + PREP_OFF) + 1, len(jobs))) for a in needs[m] if a not in ready]
                 if ahead:
                     prepare(ahead[0])
                 jobs[n][0]()
                 count["issued"] += 1
+
+        later = []
+
+        def flush():
+            while later:
+                dst, src = later[0]
+                later.remove(later[0])
+                nc.vector.tensor_copy(out=dst, in_=src)
+
+        def last_of(x):
+            return jobs_of[min(x, NX - 1)][-1] + 1
 
         for s in range(-A, NX + Q + O):
             mine = jobs_of.get(s + A, [])
@@ -335,7 +358,10 @@ def tile_scaleddotproductattention_kernel(tc, q, k, v, is_causal, out):
                 at(n, len(mine))
                 issue(jb + 1)
                 jobs[jb][1]()
-                issue(jb + 1 + LOOKAHEAD)
+                issue(min(jb + 1 + LOOKAHEAD, last_of(s + A + TL)))
+                if n == VC_POS:
+                    flush()
+            flush()
             at(len(mine), len(mine))
             if s in V_STEPS:
                 v_regroup(*V_STEPS[s])

@@ -30,18 +30,20 @@ PV_BANKS = 2
 LOOKAHEAD = 3
 A = 2
 C = 1
-Q = 3
+Q = 4
 O = 1
 TPOS = (0, 0)
-PPOS = 0
+PPOS = 1
 QPOS = 0
 OPOS = 9
 OUT_S = 0
-VCOPY = tuple((1, i, j, 1) for i in (2, 3) for j in (0, 2))
-V_STEPS = {0: (0, 0), 4: (0, 1), 10: (1, 1), 12: (1, 0)}
+VCOPY = ()
+V_STEPS = {0: (0, 0), 3: (0, 1), 7: (0, 2), 11: (0, 3), 12: (1, 0), 13: (1, 1), 14: (1, 2), 15: (1, 3)}
 PREP_AHEAD = 1
 PREP_OFF = 0
 TL = 1
+PREP1 = {1: [("k", 0, 1), ("q", 0, 1)], 3: [("q", 0, 2)], 4: [("k", 0, 2)], 6: [("k", 0, 3)], 7: [("q", 0, 3)], 8: [("k", 1, 0)], 9: [("k", 1, 1)], 10: [("k", 1, 2)], 11: [("k", 1, 3)], 12: [("q", 1, 3)], 16: [("q", 1, 2)], 20: [("q", 1, 1)], 23: [("q", 1, 0)]}
+PREP1_POS = 0
 FIRST = ((0, 1), (1, 4))
 PREP_V = ()
 VC_POS = 9
@@ -59,7 +61,7 @@ def tile_scaleddotproductattention_kernel(tc, q, k, v, is_causal, out):
         ctx.enter_context(tc.manual_schedule())
         keep = ctx.enter_context(tc.tile_pool(name="keep", bufs=1))
         sneg_pool = ctx.enter_context(tc.tile_pool(name="sneg", bufs=4))
-        grp_pool = ctx.enter_context(tc.tile_pool(name="grp", bufs=4))
+        grp_pool = ctx.enter_context(tc.tile_pool(name="grp", bufs=5))
         code_pool = ctx.enter_context(tc.tile_pool(name="code", bufs=3))
         small = ctx.enter_context(tc.tile_pool(name="small", bufs=12))
         out_pool = ctx.enter_context(tc.tile_pool(name="outp", bufs=8))
@@ -73,14 +75,11 @@ def tile_scaleddotproductattention_kernel(tc, q, k, v, is_causal, out):
         for lo, hi in FIRST:
             nc.sync.dma_start(out=k_sb[0][:, lo:hi, :], in_=k_v[0][:, lo:hi, :])
             nc.sync.dma_start(out=q_sb[0][:, lo:hi, :], in_=q_v[0][:, lo:hi, :])
-        nc.sync.dma_start(out=k_sb[0][:, 4:8, :], in_=k_v[0][:, 4:8, :])
-        nc.sync.dma_start(out=q_sb[0][:, 4:8, :], in_=q_v[0][:, 4:8, :])
-        nc.sync.dma_start(out=v_sb[0][:, 0:2, :], in_=v_v[0][:, 0:2, :])
-        nc.sync.dma_start(out=k_sb[0][:, 8:12, :], in_=k_v[0][:, 8:12, :])
-        nc.sync.dma_start(out=q_sb[0][:, 8:12, :], in_=q_v[0][:, 8:12, :])
-        nc.sync.dma_start(out=v_sb[0][:, 2:4, :], in_=v_v[0][:, 2:4, :])
-        nc.sync.dma_start(out=k_sb[0][:, 12:NT, :], in_=k_v[0][:, 12:NT, :])
-        nc.sync.dma_start(out=q_sb[0][:, 12:NT, :], in_=q_v[0][:, 12:NT, :])
+        for g in range(4):
+            if g > 0:
+                nc.sync.dma_start(out=k_sb[0][:, 4 * g:4 * g + 4, :], in_=k_v[0][:, 4 * g:4 * g + 4, :])
+                nc.sync.dma_start(out=q_sb[0][:, 4 * g:4 * g + 4, :], in_=q_v[0][:, 4 * g:4 * g + 4, :])
+            nc.sync.dma_start(out=v_sb[0][:, g, :], in_=v_v[0][:, g, :])
         nc.sync.dma_start(out=k_sb[1][:], in_=k_v[1])
         nc.sync.dma_start(out=q_sb[1][:], in_=q_v[1])
         nc.sync.dma_start(out=v_sb[1][:], in_=v_v[1])
@@ -209,18 +208,17 @@ def tile_scaleddotproductattention_kernel(tc, q, k, v, is_causal, out):
                 width.append(t // 4 + 1)
             jobs_of[x] = mine
 
-        def v_regroup(h, half):
-            gs = slice(2 * half, 2 * half + 2)
+        def v_regroup(h, g):
             nc.gpsimd.tensor_scalar(
-                out=v_grp[h][:, gs], in0=v_sb[h][:, gs, :].rearrange("p g (t d) -> p g d t", t=4),
+                out=v_grp[h][:, g], in0=v_sb[h][:, g, :].rearrange("p (t d) -> p d t", t=4),
                 scalar1=1.0, scalar2=0.0, op0=ALU.mult, op1=ALU.add,
             )
 
-        def v_quant(h, half):
-            cols = slice(2 * D * half, 2 * D * (half + 1))
+        def v_quant(h, g):
+            cols = slice(D * g, D * (g + 1))
             nc.vector.quantize_mx(
                 out=v_codes[h][:, cols].bitcast(FP8X4), scales=v_scales[h][:, cols],
-                in_=v_grp[h][:, 2 * half:2 * half + 2].rearrange("p g d t -> p (g d t)"),
+                in_=v_grp[h][:, g].rearrange("p d t -> p (d t)"),
             )
 
         def exp_stage(x):
@@ -356,6 +354,10 @@ def tile_scaleddotproductattention_kernel(tc, q, k, v, is_causal, out):
                 exp_stage(s)
             for n, jb in enumerate(mine):
                 at(n, len(mine))
+                if n == min(PREP1_POS, len(mine) - 1):
+                    for args in PREP1.get(s, []):
+                        if args not in ready:
+                            prepare(args)
                 issue(jb + 1)
                 jobs[jb][1]()
                 issue(min(jb + 1 + LOOKAHEAD, last_of(s + A + TL)))

@@ -37,7 +37,7 @@ PPOS = 1
 QPOS = 0
 OPOS = 9
 OUT_S = 0
-VCOPY = ()
+VCOPY = tuple((1, i, j, 1) for i in (2, 3) for j in (0, 2))
 V_STEPS = {0: (0, 0), 3: (0, 1), 7: (0, 2), 11: (0, 3), 12: (1, 0), 13: (1, 1), 14: (1, 2), 15: (1, 3)}
 PREP_AHEAD = 1
 PREP_OFF = 0

@@ -10,43 +10,28 @@ U8 = mybir.dt.uint8
 FP8X4 = mybir.dt.float8_e4m3fn_x4
 ALU = mybir.AluOpType
 ACT = mybir.ActivationFunctionType
-AX = mybir.AxisListType
 
 P = 128
 H = 2
 S = 2048
 D = 128
 NT = S // P
-PASS = 512
+NG = 4
+PASS = S // NG
 HALF = PASS // 2
 SH = S // 2
 SCALE = 1.0 / (D ** 0.5)
 MASK_VALUE = -1.0e30
-FLOPS = 4 * H * D * sum(PASS * PASS * (i + 1) for i in range(S // PASS))
+FLOPS = 4 * H * D * sum(PASS * PASS * (i + 1) for i in range(NG))
 
 S_BANKS = 3
-XT_BANKS = 3
-PV_BANKS = 2
-LOOKAHEAD = 3
-A = 2
-C = 1
-Q = 4
-O = 1
-TPOS = (0, 0)
-PPOS = 1
-QPOS = 0
-OPOS = 9
-OUT_S = 0
-VCOPY = tuple((1, i, j, 1) for i in (2, 3) for j in (0, 2))
-V_STEPS = {0: (0, 0), 3: (0, 1), 7: (0, 2), 11: (0, 3), 12: (1, 0), 13: (1, 1), 14: (1, 2), 15: (1, 3)}
-PREP_AHEAD = 1
-PREP_OFF = 0
-TL = 1
-PREP1 = {1: [("k", 0, 1), ("q", 0, 1)], 3: [("q", 0, 2)], 4: [("k", 0, 2)], 6: [("k", 0, 3)], 7: [("q", 0, 3)], 8: [("k", 1, 0)], 9: [("k", 1, 1)], 10: [("k", 1, 2)], 11: [("k", 1, 3)], 12: [("q", 1, 3)], 16: [("q", 1, 2)], 20: [("q", 1, 1)], 23: [("q", 1, 0)]}
-PREP1_POS = 0
+X_BANKS = 3
+O_BANKS = 2
+SCORES_AHEAD = 2
+QUANT_BEHIND = 4
+PREP_LEAD = 4
+V_LEAD = 3
 FIRST = ((0, 1), (1, 4))
-PREP_V = ()
-VC_POS = 9
 
 
 def tile_scaleddotproductattention_kernel(tc, q, k, v, is_causal, out):
@@ -61,21 +46,21 @@ def tile_scaleddotproductattention_kernel(tc, q, k, v, is_causal, out):
         ctx.enter_context(tc.manual_schedule())
         keep = ctx.enter_context(tc.tile_pool(name="keep", bufs=1))
         sneg_pool = ctx.enter_context(tc.tile_pool(name="sneg", bufs=4))
-        grp_pool = ctx.enter_context(tc.tile_pool(name="grp", bufs=5))
+        grp_pool = ctx.enter_context(tc.tile_pool(name="grp", bufs=QUANT_BEHIND + 1))
         code_pool = ctx.enter_context(tc.tile_pool(name="code", bufs=3))
         small = ctx.enter_context(tc.tile_pool(name="small", bufs=12))
         out_pool = ctx.enter_context(tc.tile_pool(name="outp", bufs=8))
         psum_s = ctx.enter_context(tc.psum_pool(name="ps_s", bufs=S_BANKS))
-        psum_x = ctx.enter_context(tc.psum_pool(name="ps_x", bufs=XT_BANKS))
-        psum_o = ctx.enter_context(tc.psum_pool(name="ps_o", bufs=PV_BANKS))
+        psum_x = ctx.enter_context(tc.psum_pool(name="ps_x", bufs=X_BANKS))
+        psum_o = ctx.enter_context(tc.psum_pool(name="ps_o", bufs=O_BANKS))
 
         q_sb = [keep.tile([P, NT, D], BF16, name="q_sb%d" % h) for h in range(H)]
         k_sb = [keep.tile([P, NT, D], BF16, name="k_sb%d" % h) for h in range(H)]
-        v_sb = [keep.tile([P, 4, 4 * D], BF16, name="v_sb%d" % h) for h in range(H)]
+        v_sb = [keep.tile([P, NG, 4 * D], BF16, name="v_sb%d" % h) for h in range(H)]
         for lo, hi in FIRST:
             nc.sync.dma_start(out=k_sb[0][:, lo:hi, :], in_=k_v[0][:, lo:hi, :])
             nc.sync.dma_start(out=q_sb[0][:, lo:hi, :], in_=q_v[0][:, lo:hi, :])
-        for g in range(4):
+        for g in range(NG):
             if g > 0:
                 nc.sync.dma_start(out=k_sb[0][:, 4 * g:4 * g + 4, :], in_=k_v[0][:, 4 * g:4 * g + 4, :])
                 nc.sync.dma_start(out=q_sb[0][:, 4 * g:4 * g + 4, :], in_=q_v[0][:, 4 * g:4 * g + 4, :])
@@ -99,116 +84,164 @@ def tile_scaleddotproductattention_kernel(tc, q, k, v, is_causal, out):
             out=mask_b[:].rearrange("p u (a e) -> p u a e", e=2),
             in_=mask_f[:].rearrange("p (a u e) -> p u a e", u=2, e=2),
         )
-        warm = keep.tile([P, 1], F32, name="warm")
-        nc.vector.memset(warm[:], 0.0)
-        warm2 = keep.tile([P, 1], F32, name="warm2")
-        nc.scalar.activation(out=warm2[:], in_=warm[:], func=ACT.Exp)
-        e_cls = [keep.tile([P, 2, SH], BF16, name="e_cls%d" % c) for c in range(4 * H)]
-        for c in range(4 * H):
-            if c % 4 < 3:
-                nc.gpsimd.memset(e_cls[c][:, :, SH - 64 * (3 - c % 4):SH], 0.0)
+        neg1 = keep.tile([P, 2], F32, name="neg1")
+        nc.gpsimd.memset(neg1[:], -1.0)
+        warm_in = keep.tile([P, 1], F32, name="warm_in")
+        nc.vector.memset(warm_in[:], 0.0)
+        warm_out = keep.tile([P, 1], F32, name="warm_out")
+        nc.scalar.activation(out=warm_out[:], in_=warm_in[:], func=ACT.Exp)
+        e_tiles = [[keep.tile([P, 2, SH], BF16, name="e%d_%d" % (h, j)) for j in range(4)] for h in range(H)]
+        for h in range(H):
+            for j in range(3):
+                nc.gpsimd.memset(e_tiles[h][j][:, :, SH - 64 * (3 - j):SH], 0.0)
 
         q_t = [keep.tile([P, S], BF16, name="q_t%d" % h) for h in range(H)]
         k_t = [keep.tile([P, 2, SH], BF16, name="k_t%d" % h) for h in range(H)]
-        v_grp = [keep.tile([P, 4, D, 4], BF16, name="v_grp%d" % h, align_bytes=64) for h in range(H)]
-        v_codes = [keep.tile([P, 4 * D], U32, name="v_codes%d" % h, align_bytes=64) for h in range(H)]
-        v_scales = [keep.tile([P, 4 * D], U8, name="v_scales%d" % h, align_bytes=64) for h in range(H)]
-
-        ready = set()
-        state = {}
-
-        def prep_job(kind, h, grp, lo=0, hi=4):
-            src = (k_sb if kind == "k" else q_sb)[h]
-            box = {}
-
-            def pe():
-                ps = psum_x.tile([P, 4, P], BF16, name="prep_ps", tag="x")
-                box["ps"] = ps
-                for c in range(lo, hi):
-                    nc.tensor.transpose(out=ps[:, c, :], in_=src[:, 4 * grp + c, :], identity=ident[:])
-
-            def ve():
-                words = box["ps"][:, lo:hi, :].rearrange("p c x -> p (c x)").bitcast(F32)
-                copy = nc.vector.tensor_copy if (kind, h, grp) == ("k", 0, 0) or (kind, h, grp) in PREP_V else nc.scalar.copy
-                if kind == "k":
-                    copy(
-                        out=k_t[h][:, :, HALF * grp + 64 * lo:HALF * grp + 64 * hi].bitcast(F32),
-                        in_=words.rearrange("p (a u) -> p u a", u=2),
-                    )
-                else:
-                    copy(out=q_t[h][:, PASS * grp + P * lo:PASS * grp + P * hi].bitcast(F32), in_=words)
-                ready.add((kind, h, grp))
-
-            return (pe, ve)
-
-        def qk_job(x, h, t, b):
-            i = t // 4
-            j = t % 4
-            hw = HALF if b < i else 64 * (j + 1)
-            box = {}
-
-            def pe():
-                assert ("q", h, i) in ready and all(("k", h, g) in ready for g in range(b + 1))
-                ps = psum_s.tile([P, PASS], F32, name="s_ps", tag="s")
-                view = ps[:, 0:2 * hw].rearrange("p (u n) -> p u n", u=2)
-                box["view"] = view
-                q_cols = q_t[h][:, P * t:P * (t + 1)]
-                k0 = HALF * b
-                if b < i:
-                    nc.tensor.matmul(out=view, lhsT=q_cols, rhs=k_t[h][:, :, k0:k0 + HALF], start=True, stop=True)
-                else:
-                    d0 = 64 * j
-                    if j > 0:
-                        nc.tensor.matmul(out=view[:, :, 0:d0], lhsT=q_cols, rhs=k_t[h][:, :, k0:k0 + d0], start=True, stop=True)
-                    nc.tensor.matmul(out=view[:, :, d0:d0 + 64], lhsT=q_cols, rhs=k_t[h][:, :, k0 + d0:k0 + d0 + 64], start=True, stop=False)
-                    nc.tensor.matmul(out=view[:, :, d0:d0 + 64], lhsT=ident[:], rhs=mask_b[:], start=False, stop=True)
-
-            def ve():
-                st = state[x]
-                if b == 0:
-                    st["sneg"] = sneg_pool.tile([P, 2, SH], F32, name="sneg")
-                    st["pm"] = small.tile([P, 4], F32, name="pm")
-                nc.vector.tensor_scalar(
-                    out=st["sneg"][:, :, HALF * b:HALF * b + hw], in0=box["view"],
-                    scalar1=-SCALE, scalar2=None, op0=ALU.mult, op1=ALU.min,
-                    accum_out=st["pm"][:, b:b + 1],
-                )
-                if b == i:
-                    if i > 0:
-                        negm = small.tile([P, 1], F32, name="negm")
-                        pm = st["pm"]
-                        if i == 1:
-                            nc.gpsimd.tensor_scalar(out=negm[:], in0=pm[:, 0:1], scalar1=pm[:, 1:2], scalar2=None, op0=ALU.min)
-                        else:
-                            nc.gpsimd.tensor_scalar(out=negm[:], in0=pm[:, 0:1], scalar1=pm[:, 1:2], scalar2=pm[:, 2:3], op0=ALU.min, op1=ALU.min)
-                        if i == 3:
-                            negm3 = small.tile([P, 1], F32, name="negm3")
-                            nc.gpsimd.tensor_scalar(out=negm3[:], in0=negm[:], scalar1=pm[:, 3:4], scalar2=None, op0=ALU.min)
-                            negm = negm3
-                        st["negm"] = negm[:, 0:1]
-                    else:
-                        st["negm"] = st["pm"][:, 0:1]
-
-            return (pe, ve)
+        v_grp = [keep.tile([P, NG, D, 4], BF16, name="v_grp%d" % h, align_bytes=64) for h in range(H)]
+        v_codes = [keep.tile([P, NG * D], U32, name="v_codes%d" % h, align_bytes=64) for h in range(H)]
+        v_scales = [keep.tile([P, NG * D], U8, name="v_scales%d" % h, align_bytes=64) for h in range(H)]
 
         seq = [(0, t) for t in range(NT)] + [(1, t) for t in range(NT - 1, -1, -1)]
         NX = len(seq)
-        jobs = []
-        needs = []
-        width = []
-        jobs_of = {}
-        for x in range(NX):
-            h, t = seq[x]
-            state[x] = {"h": h, "t": t, "i": t // 4, "j": t % 4}
-            mine = []
-            for b in range(t // 4 + 1):
-                mine.append(len(jobs))
-                jobs.append(qk_job(x, h, t, b))
-                needs.append([("q", h, t // 4), ("k", h, b)])
-                width.append(t // 4 + 1)
-            jobs_of[x] = mine
+        state = [{"h": h, "t": t, "i": t // 4, "j": t % 4} for (h, t) in seq]
+        ready = set()
+        later = []
 
-        def v_regroup(h, g):
+        def prepare(kind, h, g, lo=0, hi=4):
+            src = (k_sb if kind == "k" else q_sb)[h]
+            ps = psum_x.tile([P, 4, P], BF16, name="prep", tag="x")
+            for c in range(lo, hi):
+                nc.tensor.transpose(out=ps[:, c, :], in_=src[:, 4 * g + c, :], identity=ident[:])
+            words = ps[:, lo:hi, :].rearrange("p c x -> p (c x)").bitcast(F32)
+            copy = nc.vector.tensor_copy if (kind, h, g) == ("k", 0, 0) else nc.scalar.copy
+            if kind == "k":
+                copy(
+                    out=k_t[h][:, :, HALF * g + 64 * lo:HALF * g + 64 * hi].bitcast(F32),
+                    in_=words.rearrange("p (a u) -> p u a", u=2),
+                )
+            else:
+                copy(out=q_t[h][:, PASS * g + P * lo:PASS * g + P * hi].bitcast(F32), in_=words)
+            ready.add((kind, h, g))
+
+        def width(st, b):
+            return HALF if b < st["i"] else 64 * (st["j"] + 1)
+
+        def score_matmul(x, b):
+            st = state[x]
+            h, t, j, hw = st["h"], st["t"], st["j"], width(st, b)
+            assert ("q", h, st["i"]) in ready and ("k", h, b) in ready
+            ps = psum_s.tile([P, PASS], F32, name="s_ps")
+            view = ps[:, 0:2 * hw].rearrange("p (u n) -> p u n", u=2)
+            st["ps", b] = view
+            q_cols = q_t[h][:, P * t:P * (t + 1)]
+            k0 = HALF * b
+            if b < st["i"]:
+                nc.tensor.matmul(out=view, lhsT=q_cols, rhs=k_t[h][:, :, k0:k0 + HALF], start=True, stop=True)
+            else:
+                d0 = 64 * j
+                if j > 0:
+                    nc.tensor.matmul(out=view[:, :, 0:d0], lhsT=q_cols, rhs=k_t[h][:, :, k0:k0 + d0], start=True, stop=True)
+                nc.tensor.matmul(out=view[:, :, d0:d0 + 64], lhsT=q_cols, rhs=k_t[h][:, :, k0 + d0:k0 + d0 + 64], start=True, stop=False)
+                nc.tensor.matmul(out=view[:, :, d0:d0 + 64], lhsT=ident[:], rhs=mask_b[:], start=False, stop=True)
+
+        def score_out(x, b):
+            st = state[x]
+            i, hw = st["i"], width(st, b)
+            if b == 0:
+                st["sneg"] = sneg_pool.tile([P, 2, SH], F32, name="sneg")
+                st["part"] = small.tile([P, 4], F32, name="part")
+            part = st["part"]
+            nc.vector.tensor_scalar(
+                out=st["sneg"][:, :, HALF * b:HALF * b + hw], in0=st["ps", b],
+                scalar1=-SCALE, scalar2=None, op0=ALU.mult, op1=ALU.min, accum_out=part[:, b:b + 1],
+            )
+            if b == i:
+                negm = part[:, 0:1]
+                for c in range(1, i + 1, 2):
+                    both = c + 1 <= i
+                    low = small.tile([P, 1], F32, name="low%d" % c)
+                    if both:
+                        nc.gpsimd.tensor_scalar(out=low[:], in0=negm, scalar1=part[:, c:c + 1], scalar2=part[:, c + 1:c + 2], op0=ALU.min, op1=ALU.min)
+                    else:
+                        nc.gpsimd.tensor_scalar(out=low[:], in0=negm, scalar1=part[:, c:c + 1], scalar2=None, op0=ALU.min)
+                    negm = low[:, 0:1]
+                st["negm"] = negm
+
+        def exp_stage(x):
+            st = state[x]
+            n = HALF * st["i"] + 64 * (st["j"] + 1)
+            st["c0"] = SH - HALF * (st["i"] + 1)
+            st["rowsum"] = small.tile([P, 2], F32, name="rowsum") if x % 2 == 0 else state[x - 1]["rowsum"]
+            nc.scalar.activation(
+                out=e_tiles[st["h"]][st["j"]][:, :, st["c0"]:st["c0"] + n], in_=st["sneg"][:, :, 0:n], func=ACT.Exp,
+                bias=st["negm"], scale=-1.0, accum_out=st["rowsum"][:, x % 2:x % 2 + 1],
+            )
+
+        def transpose_stage(x):
+            st = state[x]
+            e = e_tiles[st["h"]][st["j"]]
+            grouped = grp_pool.tile([P, 4, P, 2], F32, name="grouped", align_bytes=64)
+            st["grouped"] = grouped
+            for g0 in range(0, st["i"] + 1, 2):
+                n2 = min(2, st["i"] + 1 - g0)
+                xt = psum_x.tile([P, 2, 2, P], F32, name="xt", tag="x")
+                for g in range(n2):
+                    for u in range(2):
+                        col = st["c0"] + HALF * (g0 + g)
+                        nc.tensor.transpose(out=xt[:, g, u, :], in_=e[:, u, col:col + HALF].bitcast(F32), identity=ident_f[:])
+                dst = grouped[:, g0:g0 + n2, :, :]
+                src = xt[:, 0:n2, :, :].rearrange("p g u x -> p g x u")
+                if g0 == 2 and st["h"] == 1 and x % 2 == 1:
+                    later.append((dst, src))
+                else:
+                    nc.scalar.copy(out=dst, in_=src)
+
+        def vector_copies():
+            for dst, src in later:
+                nc.vector.tensor_copy(out=dst, in_=src)
+            later.clear()
+
+        def quant_stage(x):
+            st = state[x]
+            npass = st["i"] + 1
+            codes = code_pool.tile([P, 4 * P], U32, name="codes", align_bytes=64)
+            scales = code_pool.tile([P, 4 * P], U8, name="scales", align_bytes=64)
+            st["codes"] = codes
+            st["scales"] = scales
+            flat = st["grouped"][:].rearrange("p g x u -> p (g x u)").bitcast(BF16)
+            lo = 0
+            for n in ((2, 1) if npass == 3 else (npass,)):
+                nc.vector.quantize_mx(
+                    out=codes[:, P * lo:P * (lo + n)].bitcast(FP8X4), scales=scales[:, P * lo:P * (lo + n)],
+                    in_=flat[:, PASS * lo:PASS * (lo + n)],
+                )
+                lo += n
+            if x % 2 == 1:
+                recip = small.tile([P, 2], F32, name="recip")
+                state[x - 1]["recip"] = recip[:, 0:1]
+                st["recip"] = recip[:, 1:2]
+                nc.gpsimd.tensor_tensor(out=recip[:], in0=st["rowsum"][:], in1=neg1[:], op=ALU.pow)
+
+        def pv_stage(x):
+            st = state[x]
+            h = st["h"]
+            pv = psum_o.tile([P, D], F32, name="pv")
+            st["pv"] = pv
+            for g in range(st["i"] + 1):
+                cols = slice(P * g, P * (g + 1))
+                nc.tensor.matmul_mx(
+                    out=pv[:], lhsT=st["codes"][:, cols].bitcast(FP8X4), lhsT_scale=st["scales"][:, cols],
+                    rhs=v_codes[h][:, cols].bitcast(FP8X4), rhs_scale=v_scales[h][:, cols],
+                    start=(g == 0), stop=(g == st["i"]),
+                )
+
+        def out_stage(x):
+            st = state[x]
+            o_sb = out_pool.tile([P, D], F32, name="o_sb")
+            nc.vector.tensor_scalar(out=o_sb[:], in0=st["pv"][:], scalar1=st["recip"], scalar2=None, op0=ALU.mult)
+            nc.sync.dma_start(out=out_v[st["h"]][st["t"]], in_=o_sb[:])
+
+        def v_interleave(h, g):
             nc.gpsimd.tensor_scalar(
                 out=v_grp[h][:, g], in0=v_sb[h][:, g, :].rearrange("p (t d) -> p d t", t=4),
                 scalar1=1.0, scalar2=0.0, op0=ALU.mult, op1=ALU.add,
@@ -221,151 +254,62 @@ def tile_scaleddotproductattention_kernel(tc, q, k, v, is_causal, out):
                 in_=v_grp[h][:, g].rearrange("p d t -> p (d t)"),
             )
 
-        def exp_stage(x):
-            st = state[x]
-            n = HALF * st["i"] + 64 * (st["j"] + 1)
-            c0 = SH - HALF * (st["i"] + 1)
-            st["c0"] = c0
-            if x % 2 == 0:
-                st["rowsum"] = small.tile([P, 2], F32, name="rowsum")
-            else:
-                st["rowsum"] = state[x - 1]["rowsum"]
-            nc.scalar.activation(
-                out=e_cls[4 * st["h"] + st["j"]][:, :, c0:c0 + n], in_=st["sneg"][:, :, 0:n], func=ACT.Exp,
-                bias=st["negm"], scale=-1.0, accum_out=st["rowsum"][:, x % 2:x % 2 + 1],
-            )
+        def steps_of(lead, kinds):
+            first = {}
+            for x in range(NX):
+                h, i = state[x]["h"], state[x]["i"]
+                for kind in kinds:
+                    for g in (range(i, i + 1) if kind == "q" else range(i + 1)):
+                        first.setdefault((kind, h, g), x)
+            steps = {}
+            step = NX
+            for key in reversed(list(first)):
+                step = min(first[key] - lead, step - 1)
+                steps.setdefault(max(step, 0), []).append(key)
+            return steps
 
-        def transpose_stage(x, half):
-            st = state[x]
-            npass = st["i"] + 1
-            e = e_cls[4 * st["h"] + st["j"]]
-            if half == 0:
-                st["grouped"] = grp_pool.tile([P, 4, P, 2], F32, name="grouped", align_bytes=64)
-            g0 = 2 * half
-            if g0 >= npass:
-                return
-            n2 = min(2, npass - g0)
-            xt = psum_x.tile([P, 2, 2, P], F32, name="xt", tag="x")
-            for g in range(g0, g0 + n2):
-                for u in range(2):
-                    col = st["c0"] + HALF * g
-                    nc.tensor.transpose(out=xt[:, g - g0, u, :], in_=e[:, u, col:col + HALF].bitcast(F32), identity=ident_f[:])
-            dst = st["grouped"][:, g0:g0 + n2, :, :]
-            src = xt[:, 0:n2, :, :].rearrange("p g u x -> p g x u")
-            if (st["h"], st["i"], st["j"], half) in VCOPY:
-                later.append((dst, src))
-            else:
-                nc.scalar.copy(out=dst, in_=src)
+        qk_steps = steps_of(PREP_LEAD, "qk")
+        v_steps = steps_of(V_LEAD - QUANT_BEHIND, "v")
 
-        def quant_stage(x):
-            st = state[x]
-            npass = st["i"] + 1
-            codes = code_pool.tile([P, 4 * P], U32, name="codes", align_bytes=64)
-            scales = code_pool.tile([P, 4 * P], U8, name="scales", align_bytes=64)
-            st["codes"] = codes
-            st["scales"] = scales
-            flat = st["grouped"][:].rearrange("p g x u -> p (g x u)").bitcast(BF16)
-            a = 0
-            for wd in {1: [1], 2: [2], 3: [2, 1], 4: [4]}[npass]:
-                nc.vector.quantize_mx(
-                    out=codes[:, P * a:P * (a + wd)].bitcast(FP8X4), scales=scales[:, P * a:P * (a + wd)],
-                    in_=flat[:, PASS * a:PASS * (a + wd)],
-                )
-                a += wd
-            if x % 2 == 1:
-                recip = small.tile([P, 2], F32, name="recip")
-                st["recip"] = recip[:, 1:2]
-                state[x - 1]["recip"] = recip[:, 0:1]
-                nc.vector.reciprocal(out=recip[:], in_=st["rowsum"][:])
+        jobs = [(x, b) for x in range(NX) for b in range(state[x]["i"] + 1)]
+        issued = []
 
-        def pv_stage(x):
-            st = state[x]
-            npass = st["i"] + 1
-            h = st["h"]
-            pv = psum_o.tile([P, D], F32, name="pv")
-            st["pv"] = pv
-            for g in range(npass):
-                cols = slice(P * g, P * (g + 1))
-                nc.tensor.matmul_mx(
-                    out=pv[:], lhsT=st["codes"][:, cols].bitcast(FP8X4), lhsT_scale=st["scales"][:, cols],
-                    rhs=v_codes[h][:, cols].bitcast(FP8X4), rhs_scale=v_scales[h][:, cols],
-                    start=(g == 0), stop=(g == npass - 1),
-                )
+        def issue(upto, newest_tile):
+            while len(issued) < min(upto, len(jobs)) and jobs[len(issued)][0] <= newest_tile:
+                x, b = jobs[len(issued)]
+                for kind, g in (("q", state[x]["i"]), ("k", b)):
+                    if (kind, state[x]["h"], g) not in ready:
+                        prepare(kind, state[x]["h"], g)
+                score_matmul(x, b)
+                issued.append((x, b))
 
-        def out_stage(x):
-            st = state[x]
-            o_sb = out_pool.tile([P, D], F32, name="o_sb")
-            if OUT_S and st["h"] == 0 and x % OUT_S == 0:
-                nc.scalar.activation(out=o_sb[:], in_=st["pv"][:], func=ACT.Copy, scale=st["recip"])
-            else:
-                nc.vector.tensor_scalar(out=o_sb[:], in0=st["pv"][:], scalar1=st["recip"], scalar2=None, op0=ALU.mult)
-            nc.sync.dma_start(out=out_v[st["h"]][st["t"]], in_=o_sb[:])
-
-        first = [prep_job(kind, 0, 0, lo, hi) for (lo, hi) in FIRST for kind in ("k", "q")]
-        for pe, ve in first:
-            pe()
-            ve()
-        count = {"issued": 0}
-
-        def prepare(args):
-            pe, ve = prep_job(*args)
-            pe()
-            ve()
-
-        def issue(upto):
-            while count["issued"] < min(upto, len(jobs)):
-                n = count["issued"]
-                for args in needs[n]:
-                    if args not in ready:
-                        prepare(args)
-                ahead = [a for m in range(n, min(n + max(0, PREP_AHEAD * width[n] + PREP_OFF) + 1, len(jobs))) for a in needs[m] if a not in ready]
-                if ahead:
-                    prepare(ahead[0])
-                jobs[n][0]()
-                count["issued"] += 1
-
-        later = []
-
-        def flush():
-            while later:
-                dst, src = later[0]
-                later.remove(later[0])
-                nc.vector.tensor_copy(out=dst, in_=src)
-
-        def last_of(x):
-            return jobs_of[min(x, NX - 1)][-1] + 1
-
-        for s in range(-A, NX + Q + O):
-            mine = jobs_of.get(s + A, [])
-
-            def at(pos, n):
-                last = pos == n
-                for half in range(2):
-                    if (TPOS[half] == pos or (last and TPOS[half] > n)) and 0 <= s - C < NX:
-                        transpose_stage(s - C, half)
-                if (QPOS == pos or (last and QPOS > n)) and 0 <= s - Q < NX:
-                    quant_stage(s - Q)
-                if (PPOS == pos or (last and PPOS > n)) and 0 <= s - Q < NX:
-                    pv_stage(s - Q)
-                if (OPOS == pos or (last and OPOS > n)) and 0 <= s - Q - O < NX:
-                    out_stage(s - Q - O)
-
+        for lo, hi in FIRST:
+            for kind in "kq":
+                prepare(kind, 0, 0, lo, hi)
+        for s in range(-SCORES_AHEAD, NX + QUANT_BEHIND + 1):
             if 0 <= s < NX:
                 exp_stage(s)
-            for n, jb in enumerate(mine):
-                at(n, len(mine))
-                if n == min(PREP1_POS, len(mine) - 1):
-                    for args in PREP1.get(s, []):
-                        if args not in ready:
-                            prepare(args)
-                issue(jb + 1)
-                jobs[jb][1]()
-                issue(min(jb + 1 + LOOKAHEAD, last_of(s + A + TL)))
-                if n == VC_POS:
-                    flush()
-            flush()
-            at(len(mine), len(mine))
-            if s in V_STEPS:
-                v_regroup(*V_STEPS[s])
-            if s - 1 in V_STEPS:
-                v_quant(*V_STEPS[s - 1])
+            if 0 <= s - 1 < NX:
+                transpose_stage(s - 1)
+            if 0 <= s - QUANT_BEHIND < NX:
+                quant_stage(s - QUANT_BEHIND)
+            for kind, h, g in qk_steps.get(s, []):
+                if (kind, h, g) not in ready:
+                    prepare(kind, h, g)
+            ahead = s + SCORES_AHEAD
+            mine = [n for n, (x, b) in enumerate(jobs) if x == ahead]
+            for n in mine:
+                issue(n + 1, ahead)
+                score_out(*jobs[n])
+                issue(n + 1 + S_BANKS, ahead + 1)
+                if n == mine[0] and 0 <= s - QUANT_BEHIND < NX:
+                    pv_stage(s - QUANT_BEHIND)
+            if not mine and 0 <= s - QUANT_BEHIND < NX:
+                pv_stage(s - QUANT_BEHIND)
+            vector_copies()
+            if 0 <= s - QUANT_BEHIND - 1 < NX:
+                out_stage(s - QUANT_BEHIND - 1)
+            for kind, h, g in v_steps.get(s, []):
+                v_interleave(h, g)
+            for kind, h, g in v_steps.get(s - 1, []):
+                v_quant(h, g)

@@ -69,6 +69,12 @@ def tile_scaleddotproductattention_kernel(tc, q, k, v, is_causal, out):
         nc.sync.dma_start(out=q_sb[1][:], in_=q_v[1])
         nc.sync.dma_start(out=v_sb[1][:], in_=v_v[1])
 
+        zero = keep.tile([P, PASS], BF16, name="zero")
+        nc.vector.memset(zero[:], 0.0)
+        idle = psum_o.tile([P, PASS], F32, name="pv")
+        for n in range(6):
+            nc.tensor.matmul(out=idle[:], lhsT=zero[:, 0:P], rhs=zero[:], start=True, stop=True)
+
         ident = keep.tile([P, P], BF16, name="ident")
         masks.make_identity(nc, ident[:])
         mask_f = keep.tile([P, P], F32, name="mask_f")
@@ -84,8 +90,6 @@ def tile_scaleddotproductattention_kernel(tc, q, k, v, is_causal, out):
             out=mask_b[:].rearrange("p u (a e) -> p u a e", e=2),
             in_=mask_f[:].rearrange("p (a u e) -> p u a e", u=2, e=2),
         )
-        neg1 = keep.tile([P, 2], F32, name="neg1")
-        nc.gpsimd.memset(neg1[:], -1.0)
         warm_in = keep.tile([P, 1], F32, name="warm_in")
         nc.vector.memset(warm_in[:], 0.0)
         warm_out = keep.tile([P, 1], F32, name="warm_out")
@@ -220,7 +224,7 @@ def tile_scaleddotproductattention_kernel(tc, q, k, v, is_causal, out):
                 recip = small.tile([P, 2], F32, name="recip")
                 state[x - 1]["recip"] = recip[:, 0:1]
                 st["recip"] = recip[:, 1:2]
-                nc.gpsimd.tensor_tensor(out=recip[:], in0=st["rowsum"][:], in1=neg1[:], op=ALU.pow)
+                nc.vector.reciprocal(out=recip[:], in_=st["rowsum"][:])
 
         def pv_stage(x):
             st = state[x]

@@ -72,7 +72,7 @@ def tile_scaleddotproductattention_kernel(tc, q, k, v, is_causal, out):
         zero = keep.tile([P, PASS], BF16, name="zero")
         nc.vector.memset(zero[:], 0.0)
         idle = psum_o.tile([P, PASS], F32, name="pv")
-        for n in range(6):
+        for n in range(3):
             nc.tensor.matmul(out=idle[:], lhsT=zero[:, 0:P], rhs=zero[:], start=True, stop=True)
 
         ident = keep.tile([P, P], BF16, name="ident")

from contextlib import ExitStack

import concourse.masks as masks
import concourse.mybir as mybir

F32 = mybir.dt.float32
BF16 = mybir.dt.bfloat16
U32 = mybir.dt.uint32
U8 = mybir.dt.uint8
FP8X4 = mybir.dt.float8_e4m3fn_x4
ALU = mybir.AluOpType
ACT = mybir.ActivationFunctionType

P = 128
H = 2
S = 2048
D = 128
NT = S // P
NG = 4
PASS = S // NG
HALF = PASS // 2
SH = S // 2
SCALE = 1.0 / (D ** 0.5)
MASK_VALUE = -1.0e30
FLOPS = 4 * H * D * sum(PASS * PASS * (i + 1) for i in range(NG))

S_BANKS = 3
X_BANKS = 3
O_BANKS = 2
SCORES_AHEAD = 2
QUANT_BEHIND = 4
PREP_LEAD = 4
V_LEAD = 3
FIRST = ((0, 1), (1, 4))


def tile_scaleddotproductattention_kernel(tc, q, k, v, is_causal, out):
    nc = tc.nc
    assert is_causal == 1
    q_v = q.rearrange("b h (c p) d -> (b h) p c d", p=P)
    k_v = k.rearrange("b h (c p) d -> (b h) p c d", p=P)
    v_v = v.rearrange("b h (g p t) d -> (b h) p g (t d)", p=P, t=4)
    out_v = out.rearrange("b h (c p) d -> (b h) c p d", p=P)

    with ExitStack() as ctx:
        ctx.enter_context(tc.manual_schedule())
        keep = ctx.enter_context(tc.tile_pool(name="keep", bufs=1))
        sneg_pool = ctx.enter_context(tc.tile_pool(name="sneg", bufs=4))
        grp_pool = ctx.enter_context(tc.tile_pool(name="grp", bufs=QUANT_BEHIND + 1))
        code_pool = ctx.enter_context(tc.tile_pool(name="code", bufs=3))
        small = ctx.enter_context(tc.tile_pool(name="small", bufs=12))
        out_pool = ctx.enter_context(tc.tile_pool(name="outp", bufs=8))
        psum_s = ctx.enter_context(tc.psum_pool(name="ps_s", bufs=S_BANKS))
        psum_x = ctx.enter_context(tc.psum_pool(name="ps_x", bufs=X_BANKS))
        psum_o = ctx.enter_context(tc.psum_pool(name="ps_o", bufs=O_BANKS))

        q_sb = [keep.tile([P, NT, D], BF16, name="q_sb%d" % h) for h in range(H)]
        k_sb = [keep.tile([P, NT, D], BF16, name="k_sb%d" % h) for h in range(H)]
        v_sb = [keep.tile([P, NG, 4 * D], BF16, name="v_sb%d" % h) for h in range(H)]
        for lo, hi in FIRST:
            nc.sync.dma_start(out=k_sb[0][:, lo:hi, :], in_=k_v[0][:, lo:hi, :])
            nc.sync.dma_start(out=q_sb[0][:, lo:hi, :], in_=q_v[0][:, lo:hi, :])
        for g in range(NG):
            if g > 0:
                nc.sync.dma_start(out=k_sb[0][:, 4 * g:4 * g + 4, :], in_=k_v[0][:, 4 * g:4 * g + 4, :])
                nc.sync.dma_start(out=q_sb[0][:, 4 * g:4 * g + 4, :], in_=q_v[0][:, 4 * g:4 * g + 4, :])
            nc.sync.dma_start(out=v_sb[0][:, g, :], in_=v_v[0][:, g, :])
        nc.sync.dma_start(out=k_sb[1][:], in_=k_v[1])
        nc.sync.dma_start(out=q_sb[1][:], in_=q_v[1])
        nc.sync.dma_start(out=v_sb[1][:], in_=v_v[1])

        zero = keep.tile([P, PASS], BF16, name="zero")
        nc.vector.memset(zero[:], 0.0)
        idle = psum_o.tile([P, PASS], F32, name="pv")
        for n in range(3):
            nc.tensor.matmul(out=idle[:], lhsT=zero[:, 0:P], rhs=zero[:], start=True, stop=True)

        ident = keep.tile([P, P], BF16, name="ident")
        masks.make_identity(nc, ident[:])
        mask_f = keep.tile([P, P], F32, name="mask_f")
        nc.gpsimd.memset(mask_f[:], 0.0)
        nc.gpsimd.affine_select(
            out=mask_f[:], in_=mask_f[:], compare_op=ALU.is_ge, fill=MASK_VALUE,
            base=0, pattern=[[-1, P]], channel_multiplier=1,
        )
        ident_f = keep.tile([P, P], F32, name="ident_f")
        masks.make_identity(nc, ident_f[:])
        mask_b = keep.tile([P, 2, P // 2], BF16, name="mask_b")
        nc.vector.tensor_copy(
            out=mask_b[:].rearrange("p u (a e) -> p u a e", e=2),
            in_=mask_f[:].rearrange("p (a u e) -> p u a e", u=2, e=2),
        )
        warm_in = keep.tile([P, 1], F32, name="warm_in")
        nc.vector.memset(warm_in[:], 0.0)
        warm_out = keep.tile([P, 1], F32, name="warm_out")
        nc.scalar.activation(out=warm_out[:], in_=warm_in[:], func=ACT.Exp)
        e_tiles = [[keep.tile([P, 2, SH], BF16, name="e%d_%d" % (h, j)) for j in range(4)] for h in range(H)]
        for h in range(H):
            for j in range(3):
                nc.gpsimd.memset(e_tiles[h][j][:, :, SH - 64 * (3 - j):SH], 0.0)

        q_t = [keep.tile([P, S], BF16, name="q_t%d" % h) for h in range(H)]
        k_t = [keep.tile([P, 2, SH], BF16, name="k_t%d" % h) for h in range(H)]
        v_grp = [keep.tile([P, NG, D, 4], BF16, name="v_grp%d" % h, align_bytes=64) for h in range(H)]
        v_codes = [keep.tile([P, NG * D], U32, name="v_codes%d" % h, align_bytes=64) for h in range(H)]
        v_scales = [keep.tile([P, NG * D], U8, name="v_scales%d" % h, align_bytes=64) for h in range(H)]

        seq = [(0, t) for t in range(NT)] + [(1, t) for t in range(NT - 1, -1, -1)]
        NX = len(seq)
        state = [{"h": h, "t": t, "i": t // 4, "j": t % 4} for (h, t) in seq]
        ready = set()
        later = []

        def prepare(kind, h, g, lo=0, hi=4):
            src = (k_sb if kind == "k" else q_sb)[h]
            ps = psum_x.tile([P, 4, P], BF16, name="prep", tag="x")
            for c in range(lo, hi):
                nc.tensor.transpose(out=ps[:, c, :], in_=src[:, 4 * g + c, :], identity=ident[:])
            words = ps[:, lo:hi, :].rearrange("p c x -> p (c x)").bitcast(F32)
            copy = nc.vector.tensor_copy if (kind, h, g) == ("k", 0, 0) else nc.scalar.copy
            if kind == "k":
                copy(
                    out=k_t[h][:, :, HALF * g + 64 * lo:HALF * g + 64 * hi].bitcast(F32),
                    in_=words.rearrange("p (a u) -> p u a", u=2),
                )
            else:
                copy(out=q_t[h][:, PASS * g + P * lo:PASS * g + P * hi].bitcast(F32), in_=words)
            ready.add((kind, h, g))

        def width(st, b):
            return HALF if b < st["i"] else 64 * (st["j"] + 1)

        def score_matmul(x, b):
            st = state[x]
            h, t, j, hw = st["h"], st["t"], st["j"], width(st, b)
            assert ("q", h, st["i"]) in ready and ("k", h, b) in ready
            ps = psum_s.tile([P, PASS], F32, name="s_ps")
            view = ps[:, 0:2 * hw].rearrange("p (u n) -> p u n", u=2)
            st["ps", b] = view
            q_cols = q_t[h][:, P * t:P * (t + 1)]
            k0 = HALF * b
            if b < st["i"]:
                nc.tensor.matmul(out=view, lhsT=q_cols, rhs=k_t[h][:, :, k0:k0 + HALF], start=True, stop=True)
            else:
                d0 = 64 * j
                if j > 0:
                    nc.tensor.matmul(out=view[:, :, 0:d0], lhsT=q_cols, rhs=k_t[h][:, :, k0:k0 + d0], start=True, stop=True)
                nc.tensor.matmul(out=view[:, :, d0:d0 + 64], lhsT=q_cols, rhs=k_t[h][:, :, k0 + d0:k0 + d0 + 64], start=True, stop=False)
                nc.tensor.matmul(out=view[:, :, d0:d0 + 64], lhsT=ident[:], rhs=mask_b[:], start=False, stop=True)

        def score_out(x, b):
            st = state[x]
            i, hw = st["i"], width(st, b)
            if b == 0:
                st["sneg"] = sneg_pool.tile([P, 2, SH], F32, name="sneg")
                st["part"] = small.tile([P, 4], F32, name="part")
            part = st["part"]
            nc.vector.tensor_scalar(
                out=st["sneg"][:, :, HALF * b:HALF * b + hw], in0=st["ps", b],
                scalar1=-SCALE, scalar2=None, op0=ALU.mult, op1=ALU.min, accum_out=part[:, b:b + 1],
            )
            if b == i:
                negm = part[:, 0:1]
                for c in range(1, i + 1, 2):
                    both = c + 1 <= i
                    low = small.tile([P, 1], F32, name="low%d" % c)
                    if both:
                        nc.gpsimd.tensor_scalar(out=low[:], in0=negm, scalar1=part[:, c:c + 1], scalar2=part[:, c + 1:c + 2], op0=ALU.min, op1=ALU.min)
                    else:
                        nc.gpsimd.tensor_scalar(out=low[:], in0=negm, scalar1=part[:, c:c + 1], scalar2=None, op0=ALU.min)
                    negm = low[:, 0:1]
                st["negm"] = negm

        def exp_stage(x):
            st = state[x]
            n = HALF * st["i"] + 64 * (st["j"] + 1)
            st["c0"] = SH - HALF * (st["i"] + 1)
            st["rowsum"] = small.tile([P, 2], F32, name="rowsum") if x % 2 == 0 else state[x - 1]["rowsum"]
            nc.scalar.activation(
                out=e_tiles[st["h"]][st["j"]][:, :, st["c0"]:st["c0"] + n], in_=st["sneg"][:, :, 0:n], func=ACT.Exp,
                bias=st["negm"], scale=-1.0, accum_out=st["rowsum"][:, x % 2:x % 2 + 1],
            )

        def transpose_stage(x):
            st = state[x]
            e = e_tiles[st["h"]][st["j"]]
            grouped = grp_pool.tile([P, 4, P, 2], F32, name="grouped", align_bytes=64)
            st["grouped"] = grouped
            for g0 in range(0, st["i"] + 1, 2):
                n2 = min(2, st["i"] + 1 - g0)
                xt = psum_x.tile([P, 2, 2, P], F32, name="xt", tag="x")
                for g in range(n2):
                    for u in range(2):
                        col = st["c0"] + HALF * (g0 + g)
                        nc.tensor.transpose(out=xt[:, g, u, :], in_=e[:, u, col:col + HALF].bitcast(F32), identity=ident_f[:])
                dst = grouped[:, g0:g0 + n2, :, :]
                src = xt[:, 0:n2, :, :].rearrange("p g u x -> p g x u")
                if g0 == 2 and st["h"] == 1 and x % 2 == 1:
                    later.append((dst, src))
                else:
                    nc.scalar.copy(out=dst, in_=src)

        def vector_copies():
            for dst, src in later:
                nc.vector.tensor_copy(out=dst, in_=src)
            later.clear()

        def quant_stage(x):
            st = state[x]
            npass = st["i"] + 1
            codes = code_pool.tile([P, 4 * P], U32, name="codes", align_bytes=64)
            scales = code_pool.tile([P, 4 * P], U8, name="scales", align_bytes=64)
            st["codes"] = codes
            st["scales"] = scales
            flat = st["grouped"][:].rearrange("p g x u -> p (g x u)").bitcast(BF16)
            lo = 0
            for n in ((2, 1) if npass == 3 else (npass,)):
                nc.vector.quantize_mx(
                    out=codes[:, P * lo:P * (lo + n)].bitcast(FP8X4), scales=scales[:, P * lo:P * (lo + n)],
                    in_=flat[:, PASS * lo:PASS * (lo + n)],
                )
                lo += n
            if x % 2 == 1:
                recip = small.tile([P, 2], F32, name="recip")
                state[x - 1]["recip"] = recip[:, 0:1]
                st["recip"] = recip[:, 1:2]
                nc.vector.reciprocal(out=recip[:], in_=st["rowsum"][:])

        def pv_stage(x):
            st = state[x]
            h = st["h"]
            pv = psum_o.tile([P, D], F32, name="pv")
            st["pv"] = pv
            for g in range(st["i"] + 1):
                cols = slice(P * g, P * (g + 1))
                nc.tensor.matmul_mx(
                    out=pv[:], lhsT=st["codes"][:, cols].bitcast(FP8X4), lhsT_scale=st["scales"][:, cols],
                    rhs=v_codes[h][:, cols].bitcast(FP8X4), rhs_scale=v_scales[h][:, cols],
                    start=(g == 0), stop=(g == st["i"]),
                )

        def out_stage(x):
            st = state[x]
            o_sb = out_pool.tile([P, D], F32, name="o_sb")
            nc.vector.tensor_scalar(out=o_sb[:], in0=st["pv"][:], scalar1=st["recip"], scalar2=None, op0=ALU.mult)
            nc.sync.dma_start(out=out_v[st["h"]][st["t"]], in_=o_sb[:])

        def v_interleave(h, g):
            nc.gpsimd.tensor_scalar(
                out=v_grp[h][:, g], in0=v_sb[h][:, g, :].rearrange("p (t d) -> p d t", t=4),
                scalar1=1.0, scalar2=0.0, op0=ALU.mult, op1=ALU.add,
            )

        def v_quant(h, g):
            cols = slice(D * g, D * (g + 1))
            nc.vector.quantize_mx(
                out=v_codes[h][:, cols].bitcast(FP8X4), scales=v_scales[h][:, cols],
                in_=v_grp[h][:, g].rearrange("p d t -> p (d t)"),
            )

        def steps_of(lead, kinds):
            first = {}
            for x in range(NX):
                h, i = state[x]["h"], state[x]["i"]
                for kind in kinds:
                    for g in (range(i, i + 1) if kind == "q" else range(i + 1)):
                        first.setdefault((kind, h, g), x)
            steps = {}
            step = NX
            for key in reversed(list(first)):
                step = min(first[key] - lead, step - 1)
                steps.setdefault(max(step, 0), []).append(key)
            return steps

        qk_steps = steps_of(PREP_LEAD, "qk")
        v_steps = steps_of(V_LEAD - QUANT_BEHIND, "v")

        jobs = [(x, b) for x in range(NX) for b in range(state[x]["i"] + 1)]
        issued = []

        def issue(upto, newest_tile):
            while len(issued) < min(upto, len(jobs)) and jobs[len(issued)][0] <= newest_tile:
                x, b = jobs[len(issued)]
                for kind, g in (("q", state[x]["i"]), ("k", b)):
                    if (kind, state[x]["h"], g) not in ready:
                        prepare(kind, state[x]["h"], g)
                score_matmul(x, b)
                issued.append((x, b))

        for lo, hi in FIRST:
            for kind in "kq":
                prepare(kind, 0, 0, lo, hi)
        for s in range(-SCORES_AHEAD, NX + QUANT_BEHIND + 1):
            if 0 <= s < NX:
                exp_stage(s)
            if 0 <= s - 1 < NX:
                transpose_stage(s - 1)
            if 0 <= s - QUANT_BEHIND < NX:
                quant_stage(s - QUANT_BEHIND)
            for kind, h, g in qk_steps.get(s, []):
                if (kind, h, g) not in ready:
                    prepare(kind, h, g)
            ahead = s + SCORES_AHEAD
            mine = [n for n, (x, b) in enumerate(jobs) if x == ahead]
            for n in mine:
                issue(n + 1, ahead)
                score_out(*jobs[n])
                issue(n + 1 + S_BANKS, ahead + 1)
                if n == mine[0] and 0 <= s - QUANT_BEHIND < NX:
                    pv_stage(s - QUANT_BEHIND)
            if not mine and 0 <= s - QUANT_BEHIND < NX:
                pv_stage(s - QUANT_BEHIND)
            vector_copies()
            if 0 <= s - QUANT_BEHIND - 1 < NX:
                out_stage(s - QUANT_BEHIND - 1)
            for kind, h, g in v_steps.get(s, []):
                v_interleave(h, g)
            for kind, h, g in v_steps.get(s - 1, []):
                v_quant(h, g)
